import numpy as np
import ml_dtypes


def mxq(x, axis, fmt="e4m3"):
    dtype, down = {"e4m3": (ml_dtypes.float8_e4m3fn, 7), "e5m2": (ml_dtypes.float8_e5m2, 14)}[fmt]
    v = np.moveaxis(np.asarray(x, np.float32).astype(ml_dtypes.bfloat16).astype(np.float64), axis, -1)
    blocks = v.reshape(v.shape[:-1] + (-1, 32))
    amax = np.abs(blocks).max(-1, keepdims=True)
    byte = np.maximum(np.where(amax > 0, np.frexp(amax)[1] - 1 + 127, 0) - down, 1)
    scale = np.exp2(byte - 127.0)
    codes = (blocks / scale).astype(np.float32).astype(dtype).astype(np.float64)
    return np.moveaxis((codes * scale).reshape(v.shape), -1, axis)


WIDE = False


def mx_kscale(k):
    if not WIDE:
        return np.ones(k)
    levels = np.array([10, -10, 5, -5, 0])
    a = np.random.permutation(np.resize(levels, k // 512 * 4)).reshape(k // 512, 4)
    idx = np.arange(k)
    return np.exp2(a[idx // 512, idx % 128 // 32])


BF16 = ml_dtypes.bfloat16


def bf(x):
    return np.asarray(x, np.float32).astype(BF16)


def f64(x):
    return np.asarray(x).astype(np.float64)


B, SD, A, H, HS, M, C, F1, F2 = 4096, 896, 128, 512, 32, 896, 2, 512, 300
K2 = M + A
EPS = 1e-12


def l2norm(v):
    n = np.sqrt(np.sum(v * v, axis=-1, keepdims=True))
    return v / np.maximum(n, EPS)


def setup_inputs():
    s = mx_kscale(H)
    t = mx_kscale(K2)[M:]
    col = np.concatenate([np.full(M, 0.7), 0.7 / np.sqrt(A) / t])
    return {"xum": bf(np.tanh(np.random.standard_normal((B, H))) * s),
            "action": bf(np.random.standard_normal((B, A)) * t),
            "up_w3": bf(np.random.standard_normal((M, H)) * 1.5 / np.sqrt(H) / s[None, :]),
            "up_b3": bf(np.random.standard_normal(M) * 0.3),
            "dyn_w1_mu": bf(np.random.standard_normal((F1, K2)) * col[None, :]),
            "dyn_b1": bf(np.random.standard_normal(F1) * 0.3)}


def reference(xum, action, up_w3, up_b3, dyn_w1_mu, dyn_b1):
    msg_up = l2norm((mxq(f64(xum), 1, "e4m3") @ mxq(f64(up_w3), 1, "e4m3").T) + f64(up_b3))
    mu = np.concatenate([msg_up, f64(action)], axis=-1)
    return np.maximum((mxq(mu, 1, "e4m3") @ mxq(f64(dyn_w1_mu), 1, "e4m3").T) + f64(dyn_b1), 0.0)

@@ -1,0 +1,316 @@
+from contextlib import ExitStack
+
+import concourse.mybir as mybir
+from concourse.masks import make_identity
+
+F32 = mybir.dt.float32
+BF16 = mybir.dt.bfloat16
+U32 = mybir.dt.uint32
+U8 = mybir.dt.uint8
+I32 = mybir.dt.int32
+FP8X4 = mybir.dt.float8_e4m3fn_x4
+ALU = mybir.AluOpType
+ACT = mybir.ActivationFunctionType
+
+P = 128
+B, H, A, M, F1 = 4096, 512, 128, 896, 512
+NT = B // P
+NW3 = M // P
+NW1 = F1 // P
+MSG = 224
+ACO = 32
+EPS2 = 1e-24
+
+FLOPS = 2 * B * H * M + 2 * B * (M + A) * F1
+
+
+def tile_modelgraphpolicy_pb_t_kernel(tc, xum, action, up_w3, up_b3, dyn_w1_mu, dyn_b1, out):
+    nc = tc.nc
+    with ExitStack() as ctx:
+        keep = ctx.enter_context(tc.tile_pool(name="keep", bufs=1))
+        two = ctx.enter_context(tc.tile_pool(name="two", bufs=2))
+        three = ctx.enter_context(tc.tile_pool(name="three", bufs=3))
+        ps_z = ctx.enter_context(tc.psum_pool(name="ps_z", bufs=3))
+        ps_t = ctx.enter_context(tc.psum_pool(name="ps_t", bufs=3))
+        ps_o = ctx.enter_context(tc.psum_pool(name="ps_o", bufs=2))
+        ctx.enter_context(tc.manual_schedule())
+
+        ident = keep.tile([P, P], F32, name="ident")
+        ones = keep.tile([P, P], BF16, name="ones")
+        brow = keep.tile([P, 3 * 512], BF16, name="brow")
+        bias = keep.tile([P, 3 * 512], F32, name="bias")
+        neghalf = keep.tile([P, 1], F32, name="neghalf")
+        x_all = keep.tile([P, NT, H], BF16, name="x_all")
+        act_all = keep.tile([P, NT, A], BF16, name="act_all")
+        w3_raw = keep.tile([P, NW3, H], BF16, name="w3_raw")
+        w1p = keep.tile([P, NW1, 4, MSG + ACO], BF16, name="w1p")
+        w1a = keep.tile([P, NW1, A], BF16, name="w1a")
+        w3g = keep.tile([P, NW3, P, 4], BF16, name="w3g", align_bytes=64)
+        w1g = keep.tile([P, 2, F1, 4], BF16, name="w1g", align_bytes=64)
+        w3c = keep.tile([P, M], U32, name="w3c", align_bytes=64)
+        w3s = keep.tile([P, M], U8, name="w3s", align_bytes=64)
+        w1c = keep.tile([P, 2, F1], U32, name="w1c", align_bytes=64)
+        w1s = keep.tile([P, 2, F1], U8, name="w1s", align_bytes=64)
+        mu_all = keep.tile([P, NT, 4, MSG + ACO], BF16, name="mu_all")
+        xc = keep.tile([P, NT, P], U32, name="xc", align_bytes=64)
+        xs = keep.tile([P, NT, P], U8, name="xs", align_bytes=64)
+        ss = keep.tile([P, NT], F32, name="ss")
+        ssc = keep.tile([P, NT], F32, name="ssc")
+        rn = keep.tile([P, NT], F32, name="rn")
+
+        x_v = xum.rearrange("(p i) k -> p i k", i=NT)
+        a_v = action.rearrange("(p i) a -> p i a", i=NT)
+        o_v = out.rearrange("(p i) f -> p i f", i=NT)
+        w3_v = up_w3.rearrange("(j p) k -> p j k", p=P)
+
+        live = {}
+
+        def transpose_words(bank, sources):
+            for s, src in enumerate(sources):
+                nc.tensor.transpose(out=bank[:, s, :], in_=src, identity=ident[:])
+
+        def leave_bank(copy, grouped, bank, pairs):
+            copy(
+                out=grouped.bitcast(F32),
+                in_=bank[:, 0 : 2 * pairs, :].rearrange("p (a u) n -> p a n u", u=2),
+            )
+
+        def quantise(grouped, codes, scales):
+            nc.vector.quantize_mx(out=codes.bitcast(FP8X4), scales=scales, in_=grouped)
+
+        def shuffle_action(dst4, src, lo, hi):
+            dst = dst4[:].rearrange("p i (c h) m -> p (i c) h m", h=2)
+            srv = src[:].rearrange("p i (c g h j) -> p (i c) g h j", c=2, g=2, h=2)
+            for h in range(2):
+                nc.gpsimd.tensor_scalar(
+                    out=dst[:, 2 * lo : 2 * hi, h, MSG : MSG + ACO].rearrange("p a (g j) -> p a g j", g=2),
+                    in0=srv[:, 2 * lo : 2 * hi, :, h, :],
+                    scalar1=1.0,
+                    scalar2=0.0,
+                    op0=ALU.mult,
+                    op1=ALU.add,
+                )
+
+        def tr_x(k):
+            bank = ps_t.tile([P, 4, P], F32, name="tx%d" % k, tag="t")
+            transpose_words(
+                bank,
+                [x_all[:, 2 * k + a, :].bitcast(F32)[:, P * u : P * u + P] for a in range(2) for u in range(2)],
+            )
+            live["tx", k] = bank
+
+        def ex_x(k):
+            xg = two.tile([P, 2, P, 4], BF16, name="xg%d" % k, tag="xg", align_bytes=64)
+            leave_bank(nc.scalar.copy, xg[:], live["tx", k], 2)
+            live["xg", k] = xg
+
+        def q_x(k):
+            quantise(
+                live["xg", k][:].rearrange("p a n t -> p (a n t)"),
+                xc[:, 2 * k : 2 * k + 2, :].rearrange("p a n -> p (a n)"),
+                xs[:, 2 * k : 2 * k + 2, :].rearrange("p a n -> p (a n)"),
+            )
+
+        def tr_w3(k, pool, tag):
+            n = min(2, NW3 - 2 * k)
+            bank = pool.tile([P, 4, P], F32, name="tw3%d" % k, tag=tag)
+            transpose_words(
+                bank,
+                [w3_raw[:, 2 * k + a, :].bitcast(F32)[:, P * u : P * u + P] for a in range(n) for u in range(2)],
+            )
+            live["tw3", k] = bank
+
+        def ex_w3(k, copy):
+            n = min(2, NW3 - 2 * k)
+            leave_bank(copy, w3g[:, 2 * k : 2 * k + n, :, :], live["tw3", k], n)
+
+        def tr_w1(r):
+            bank = ps_o.tile([P, 4, P], F32, name="tw1%d" % r, tag="o")
+            transpose_words(bank, [w1p[:, r, u, :].bitcast(F32) for u in range(4)])
+            live["tw1", r] = bank
+
+        def ex_w1(r, copy):
+            leave_bank(copy, w1g[:, :, P * r : P * r + P, :], live["tw1", r], 2)
+
+        def stage1(i):
+            za = ps_z.tile([P, 512], F32, name="za%d" % i, tag="z")
+            zc = ps_z.tile([P, 512], F32, name="zc%d" % i, tag="z")
+            for dst, lo, hi in ((za[:, 0:512], 0, 512), (zc[:, 0:256], 512, 768), (zc[:, 256:384], 768, 896)):
+                nc.tensor.matmul_mx(
+                    out=dst,
+                    lhsT=xc[:, i, :].bitcast(FP8X4),
+                    lhsT_scale=xs[:, i, :],
+                    rhs=w3c[:, lo:hi].bitcast(FP8X4),
+                    rhs_scale=w3s[:, lo:hi],
+                    start=True,
+                    stop=True,
+                )
+            live["z", i] = (za, zc)
+
+        def add_b3(i):
+            za, zc = live["z", i]
+            zb = three.tile([P, M], F32, name="zb%d" % i, tag="zb")
+            nc.vector.tensor_tensor(out=zb[:, 0:512], in0=za[:, 0:512], in1=bias[:, 0:512], op=ALU.add)
+            nc.vector.tensor_tensor(out=zb[:, 512:896], in0=zc[:, 0:384], in1=bias[:, 512:896], op=ALU.add)
+            live["zb", i] = zb
+
+        def squares(i):
+            junk = two.tile([P, M], BF16, name="junk%d" % i, tag="junk")
+            nc.scalar.activation(out=junk[:], in_=live["zb", i][:], func=ACT.Square, accum_out=ss[:, i : i + 1])
+
+        def rnorm(i):
+            nc.gpsimd.tensor_scalar_max(out=ssc[:, i : i + 1], in0=ss[:, i : i + 1], scalar1=EPS2)
+            nc.gpsimd.tensor_tensor(out=rn[:, i : i + 1], in0=ssc[:, i : i + 1], in1=neghalf[:], op=ALU.pow)
+
+        def scale(i):
+            nc.vector.tensor_scalar(
+                out=mu_all[:, i, :, 0:MSG],
+                in0=live["zb", i][:].rearrange("p (u m) -> p u m", u=4),
+                scalar1=rn[:, i : i + 1],
+                scalar2=None,
+                op0=ALU.mult,
+            )
+
+        def tr_m(i):
+            bank = ps_t.tile([P, 4, P], F32, name="tm%d" % i, tag="t")
+            transpose_words(bank, [mu_all[:, i, u, :].bitcast(F32) for u in range(4)])
+            live["tm", i] = bank
+
+        def ex_m(i):
+            mug = two.tile([P, 2, P, 4], BF16, name="mug%d" % i, tag="mug", align_bytes=64)
+            leave_bank(nc.scalar.copy, mug[:], live["tm", i], 2)
+            live["mug", i] = mug
+
+        def q_m(i):
+            muc = three.tile([P, 2, P], U32, name="muc%d" % i, tag="muc", align_bytes=64)
+            mus = three.tile([P, 2, P], U8, name="mus%d" % i, tag="mus", align_bytes=64)
+            quantise(
+                live["mug", i][:].rearrange("p c n t -> p (c n t)"),
+                muc[:].rearrange("p c n -> p (c n)"),
+                mus[:].rearrange("p c n -> p (c n)"),
+            )
+            live["muc", i] = (muc, mus)
+
+        def stage2(i):
+            muc, mus = live["muc", i]
+            acc = ps_o.tile([P, F1], F32, name="acc%d" % i, tag="o")
+            for c in range(2):
+                nc.tensor.matmul_mx(
+                    out=acc[:],
+                    lhsT=muc[:, c, :].bitcast(FP8X4),
+                    lhsT_scale=mus[:, c, :],
+                    rhs=w1c[:, c, :].bitcast(FP8X4),
+                    rhs_scale=w1s[:, c, :],
+                    start=(c == 0),
+                    stop=(c == 1),
+                )
+            live["acc", i] = acc
+
+        def add_b1(i):
+            if i % 2 == 0:
+                live["ot", i // 2] = three.tile([P, 2, F1], F32, name="ot%d" % (i // 2), tag="ot")
+            ot = live["ot", i // 2]
+            nc.vector.tensor_tensor(out=ot[:, i % 2, :], in0=live["acc", i][:], in1=bias[:, 1024:1536], op=ALU.add)
+
+        def relu_store(i):
+            ot = live["ot", i // 2]
+            nc.scalar.activation(out=ot[:, i % 2, :], in_=ot[:, i % 2, :], func=ACT.Relu)
+            if i % 2 == 1:
+                nc.sync.dma_start(out=o_v[:, i - 1 : i + 1, :], in_=ot[:])
+
+        nc.vector.memset(brow[:].bitcast(I32), 0)
+        nc.vector.memset(ones[:], 1.0)
+        nc.vector.memset(neghalf[:], -0.5)
+        make_identity(nc, ident[:])
+
+        nc.sync.dma_start(out=x_all[:, 0:2, :], in_=x_v[:, 0:2, :])
+        nc.sync.dma_start(out=w3_raw[:, 0:4, :], in_=w3_v[:, 0:4, :])
+        nc.sync.dma_start(out=w3_raw[:, 4:7, :], in_=w3_v[:, 4:7, :])
+        nc.sync.dma_start(out=brow[0:1, 0:M], in_=up_b3.unsqueeze(0))
+        nc.sync.dma_start(out=brow[0:1, 1024:1536], in_=dyn_b1.unsqueeze(0))
+        nc.sync.dma_start(out=x_all[:, 2:4, :], in_=x_v[:, 2:4, :])
+        nc.sync.dma_start(out=act_all[:, 0:4, :], in_=a_v[:, 0:4, :])
+        for r in range(NW1):
+            nc.sync.dma_start(
+                out=w1p[:, r, :, 0:MSG],
+                in_=dyn_w1_mu[P * r : P * r + P, 0:M].rearrange("p (u m) -> p u m", u=4),
+            )
+        nc.sync.dma_start(out=w1a[:], in_=dyn_w1_mu[:, M : M + A].rearrange("(r p) a -> p r a", p=P))
+        nc.sync.dma_start(out=x_all[:, 4:8, :], in_=x_v[:, 4:8, :])
+        nc.sync.dma_start(out=act_all[:, 4:NT, :], in_=a_v[:, 4:NT, :])
+        nc.sync.dma_start(out=x_all[:, 8:16, :], in_=x_v[:, 8:16, :])
+        nc.sync.dma_start(out=x_all[:, 16:24, :], in_=x_v[:, 16:24, :])
+        nc.sync.dma_start(out=x_all[:, 24:32, :], in_=x_v[:, 24:32, :])
+
+        tr_x(0)
+        ex_x(0)
+        tr_w3(0, ps_t, "t")
+        tr_w3(1, ps_t, "t")
+        tr_w3(2, ps_z, "z")
+        tr_w3(3, ps_z, "z")
+        ex_w3(0, nc.vector.tensor_copy)
+        ex_w3(1, nc.scalar.copy)
+        ex_w3(2, nc.vector.tensor_copy)
+        ex_w3(3, nc.scalar.copy)
+        q_x(0)
+        quantise(w3g[:, 0:4, :, :].rearrange("p a n t -> p (a n t)"), w3c[:, 0:512], w3s[:, 0:512])
+        quantise(w3g[:, 4:6, :, :].rearrange("p a n t -> p (a n t)"), w3c[:, 512:768], w3s[:, 512:768])
+        quantise(w3g[:, 6:7, :, :].rearrange("p a n t -> p (a n t)"), w3c[:, 768:896], w3s[:, 768:896])
+        for b, (pool, tag, copy) in enumerate(
+            ((ps_z, "z", nc.vector.tensor_copy), (ps_o, "o", nc.scalar.copy), (ps_o, "o", nc.scalar.copy))
+        ):
+            spread = pool.tile([P, 512], F32, name="spread%d" % b, tag=tag)
+            nc.tensor.matmul(out=spread[:], lhsT=ones[:], rhs=brow[:, 512 * b : 512 * b + 512], start=True, stop=True)
+            copy(out=bias[:, 512 * b : 512 * b + 512], in_=spread[:])
+        tr_x(1)
+        ex_x(1)
+        q_x(1)
+        shuffle_action(mu_all, act_all, 0, 4)
+
+        for j in range(NT + 8):
+            if 0 <= j - 1 < NT:
+                add_b3(j - 1)
+            if 0 <= j - 7 < NT:
+                relu_store(j - 7)
+            if 0 <= j - 6 < NT:
+                add_b1(j - 6)
+            if 0 <= j - 4 < NT:
+                ex_m(j - 4)
+            if j % 2 == 0 and 2 <= (j + 2) // 2 < NT // 2:
+                ex_x((j + 2) // 2)
+            if j == 3:
+                ex_w1(0, nc.scalar.copy)
+                ex_w1(1, nc.vector.tensor_copy)
+            if j == 4:
+                ex_w1(2, nc.scalar.copy)
+                ex_w1(3, nc.vector.tensor_copy)
+            if 0 <= j - 3 < NT:
+                tr_m(j - 3)
+            if j % 2 == 1 and (j + 3) // 2 < NT // 2:
+                tr_x((j + 3) // 2)
+            if 0 <= j - 5 < NT:
+                stage2(j - 5)
+            if j < NT:
+                stage1(j)
+            if j == 2:
+                tr_w1(0)
+                tr_w1(1)
+            if j == 3:
+                tr_w1(2)
+                tr_w1(3)
+            if 0 <= j - 1 < NT:
+                squares(j - 1)
+                rnorm(j - 1)
+            if j == 1:
+                shuffle_action(w1p, w1a, 0, NW1)
+            if j % 4 == 3 and (j + 1) // 4 < NT // 4:
+                shuffle_action(mu_all, act_all, j + 1, j + 5)
+            if 0 <= j - 2 < NT:
+                scale(j - 2)
+            if j % 2 == 0 and 2 <= (j + 2) // 2 < NT // 2:
+                q_x((j + 2) // 2)
+            if j == 4:
+                for c in range(2):
+                    quantise(w1g[:, c, :, :].rearrange("p f t -> p (f t)"), w1c[:, c, :], w1s[:, c, :])
+            if 0 <= j - 4 < NT:
+                q_m(j - 4)

@@ -215,7 +215,9 @@ def tile_modelgraphpolicy_pb_t_kernel(tc, xum, action, up_w3, up_b3, dyn_w1_mu, 
         def relu_store(i):
             ot = live["ot", i // 2]
             nc.scalar.activation(out=ot[:, i % 2, :], in_=ot[:, i % 2, :], func=ACT.Relu)
-            if i % 2 == 1:
+            if i >= NT - 2:
+                nc.sync.dma_start(out=o_v[:, i : i + 1, :], in_=ot[:, i % 2 : i % 2 + 1, :])
+            elif i % 2 == 1:
                 nc.sync.dma_start(out=o_v[:, i - 1 : i + 1, :], in_=ot[:])
 
         nc.vector.memset(brow[:].bitcast(I32), 0)
@@ -267,15 +269,17 @@ def tile_modelgraphpolicy_pb_t_kernel(tc, xum, action, up_w3, up_b3, dyn_w1_mu, 
         q_x(1)
         shuffle_action(mu_all, act_all, 0, 4)
 
-        for j in range(NT + 8):
+        LS = 3
+        LT, LE, L2, LB, LR = LS + 1, LS + 2, LS + 3, LS + 4, LS + 5
+        for j in range(NT + LR + 1):
             if 0 <= j - 1 < NT:
                 add_b3(j - 1)
-            if 0 <= j - 7 < NT:
-                relu_store(j - 7)
-            if 0 <= j - 6 < NT:
-                add_b1(j - 6)
-            if 0 <= j - 4 < NT:
-                ex_m(j - 4)
+            if 0 <= j - LR < NT:
+                relu_store(j - LR)
+            if 0 <= j - LB < NT:
+                add_b1(j - LB)
+            if 0 <= j - LE < NT:
+                ex_m(j - LE)
             if j % 2 == 0 and 2 <= (j + 2) // 2 < NT // 2:
                 ex_x((j + 2) // 2)
             if j == 3:
@@ -284,12 +288,12 @@ def tile_modelgraphpolicy_pb_t_kernel(tc, xum, action, up_w3, up_b3, dyn_w1_mu, 
             if j == 4:
                 ex_w1(2, nc.scalar.copy)
                 ex_w1(3, nc.vector.tensor_copy)
-            if 0 <= j - 3 < NT:
-                tr_m(j - 3)
+            if 0 <= j - LT < NT:
+                tr_m(j - LT)
             if j % 2 == 1 and (j + 3) // 2 < NT // 2:
                 tr_x((j + 3) // 2)
-            if 0 <= j - 5 < NT:
-                stage2(j - 5)
+            if 0 <= j - L2 < NT:
+                stage2(j - L2)
             if j < NT:
                 stage1(j)
             if j == 2:
@@ -305,12 +309,12 @@ def tile_modelgraphpolicy_pb_t_kernel(tc, xum, action, up_w3, up_b3, dyn_w1_mu, 
                 shuffle_action(w1p, w1a, 0, NW1)
             if j % 4 == 3 and (j + 1) // 4 < NT // 4:
                 shuffle_action(mu_all, act_all, j + 1, j + 5)
-            if 0 <= j - 2 < NT:
-                scale(j - 2)
+            if 0 <= j - LS < NT:
+                scale(j - LS)
             if j % 2 == 0 and 2 <= (j + 2) // 2 < NT // 2:
                 q_x((j + 2) // 2)
             if j == 4:
                 for c in range(2):
                     quantise(w1g[:, c, :, :].rearrange("p f t -> p (f t)"), w1c[:, c, :], w1s[:, c, :])
-            if 0 <= j - 4 < NT:
-                q_m(j - 4)
+            if 0 <= j - LE < NT:
+                q_m(j - LE)

@@ -20,6 +20,7 @@ NW1 = F1 // P
 MSG = 224
 ACO = 32
 EPS2 = 1e-24
+FMAX = 3.4028234e38
 
 FLOPS = 2 * B * H * M + 2 * B * (M + A) * F1
 
@@ -163,6 +164,14 @@ def tile_modelgraphpolicy_pb_t_kernel(tc, xum, action, up_w3, up_b3, dyn_w1_mu, 
             nc.gpsimd.tensor_tensor(out=rn[:, i : i + 1], in0=ssc[:, i : i + 1], in1=neghalf[:], op=ALU.pow)
 
         def scale(i):
+            if i % 3 == 1:
+                nc.scalar.activation(
+                    out=mu_all[:, i, :, 0:MSG],
+                    in_=live["zb", i][:].rearrange("p (u m) -> p u m", u=4),
+                    func=ACT.Copy,
+                    scale=rn[:, i : i + 1],
+                )
+                return
             nc.vector.tensor_scalar(
                 out=mu_all[:, i, :, 0:MSG],
                 in0=live["zb", i][:].rearrange("p (u m) -> p u m", u=4),
@@ -214,7 +223,9 @@ def tile_modelgraphpolicy_pb_t_kernel(tc, xum, action, up_w3, up_b3, dyn_w1_mu, 
 
         def relu_store(i):
             ot = live["ot", i // 2]
-            nc.scalar.activation(out=ot[:, i % 2, :], in_=ot[:, i % 2, :], func=ACT.Relu)
+            nc.gpsimd.tensor_scalar(
+                out=ot[:, i % 2, :], in0=ot[:, i % 2, :], scalar1=FMAX, scalar2=0.0, op0=ALU.min, op1=ALU.max
+            )
             if i >= NT - 2:
                 nc.sync.dma_start(out=o_v[:, i : i + 1, :], in_=ot[:, i % 2 : i % 2 + 1, :])
             elif i % 2 == 1:
@@ -232,13 +243,13 @@ def tile_modelgraphpolicy_pb_t_kernel(tc, xum, action, up_w3, up_b3, dyn_w1_mu, 
         nc.sync.dma_start(out=brow[0:1, 1024:1536], in_=dyn_b1.unsqueeze(0))
         nc.sync.dma_start(out=x_all[:, 2:4, :], in_=x_v[:, 2:4, :])
         nc.sync.dma_start(out=act_all[:, 0:4, :], in_=a_v[:, 0:4, :])
+        nc.sync.dma_start(out=x_all[:, 4:8, :], in_=x_v[:, 4:8, :])
         for r in range(NW1):
             nc.sync.dma_start(
                 out=w1p[:, r, :, 0:MSG],
                 in_=dyn_w1_mu[P * r : P * r + P, 0:M].rearrange("p (u m) -> p u m", u=4),
             )
         nc.sync.dma_start(out=w1a[:], in_=dyn_w1_mu[:, M : M + A].rearrange("(r p) a -> p r a", p=P))
-        nc.sync.dma_start(out=x_all[:, 4:8, :], in_=x_v[:, 4:8, :])
         nc.sync.dma_start(out=act_all[:, 4:NT, :], in_=a_v[:, 4:NT, :])
         nc.sync.dma_start(out=x_all[:, 8:16, :], in_=x_v[:, 8:16, :])
         nc.sync.dma_start(out=x_all[:, 16:24, :], in_=x_v[:, 16:24, :])
@@ -272,48 +283,49 @@ def tile_modelgraphpolicy_pb_t_kernel(tc, xum, action, up_w3, up_b3, dyn_w1_mu, 
         LS = 3
         LT, LE, L2, LB, LR = LS + 1, LS + 2, LS + 3, LS + 4, LS + 5
         for j in range(NT + LR + 1):
-            if 0 <= j - 1 < NT:
-                add_b3(j - 1)
             if 0 <= j - LR < NT:
                 relu_store(j - LR)
+            if 0 <= j - 2 < NT:
+                rnorm(j - 2)
+            if 3 <= j <= 9:
+                shuffle_action(mu_all, act_all, 4 * (j - 2), 4 * (j - 2) + 4)
+            if 0 <= j - 1 < NT:
+                add_b3(j - 1)
             if 0 <= j - LB < NT:
                 add_b1(j - LB)
             if 0 <= j - LE < NT:
                 ex_m(j - LE)
             if j % 2 == 0 and 2 <= (j + 2) // 2 < NT // 2:
                 ex_x((j + 2) // 2)
-            if j == 3:
+            if j == 4:
                 ex_w1(0, nc.scalar.copy)
                 ex_w1(1, nc.vector.tensor_copy)
-            if j == 4:
+            if j == 5:
                 ex_w1(2, nc.scalar.copy)
                 ex_w1(3, nc.vector.tensor_copy)
             if 0 <= j - LT < NT:
                 tr_m(j - LT)
-            if j % 2 == 1 and (j + 3) // 2 < NT // 2:
-                tr_x((j + 3) // 2)
             if 0 <= j - L2 < NT:
                 stage2(j - L2)
             if j < NT:
                 stage1(j)
+            if j % 2 == 1 and (j + 3) // 2 < NT // 2:
+                tr_x((j + 3) // 2)
             if j == 2:
+                shuffle_action(w1p, w1a, 0, NW1)
+            if j == 3:
                 tr_w1(0)
                 tr_w1(1)
-            if j == 3:
+            if j == 4:
                 tr_w1(2)
                 tr_w1(3)
-            if 0 <= j - 1 < NT:
-                squares(j - 1)
-                rnorm(j - 1)
-            if j == 1:
-                shuffle_action(w1p, w1a, 0, NW1)
-            if j % 4 == 3 and (j + 1) // 4 < NT // 4:
-                shuffle_action(mu_all, act_all, j + 1, j + 5)
             if 0 <= j - LS < NT:
                 scale(j - LS)
+            if 0 <= j - 1 < NT:
+                squares(j - 1)
             if j % 2 == 0 and 2 <= (j + 2) // 2 < NT // 2:
                 q_x((j + 2) // 2)
-            if j == 4:
+            if j == 5:
                 for c in range(2):
                     quantise(w1g[:, c, :, :].rearrange("p f t -> p (f t)"), w1c[:, c, :], w1s[:, c, :])
             if 0 <= j - LE < NT:

@@ -20,7 +20,6 @@ NW1 = F1 // P
 MSG = 224
 ACO = 32
 EPS2 = 1e-24
-FMAX = 3.4028234e38
 
 FLOPS = 2 * B * H * M + 2 * B * (M + A) * F1
 
@@ -31,6 +30,7 @@ def tile_modelgraphpolicy_pb_t_kernel(tc, xum, action, up_w3, up_b3, dyn_w1_mu, 
         keep = ctx.enter_context(tc.tile_pool(name="keep", bufs=1))
         two = ctx.enter_context(tc.tile_pool(name="two", bufs=2))
         three = ctx.enter_context(tc.tile_pool(name="three", bufs=3))
+        four = ctx.enter_context(tc.tile_pool(name="four", bufs=4))
         ps_z = ctx.enter_context(tc.psum_pool(name="ps_z", bufs=3))
         ps_t = ctx.enter_context(tc.psum_pool(name="ps_t", bufs=3))
         ps_o = ctx.enter_context(tc.psum_pool(name="ps_o", bufs=2))
@@ -150,7 +150,7 @@ def tile_modelgraphpolicy_pb_t_kernel(tc, xum, action, up_w3, up_b3, dyn_w1_mu, 
 
         def add_b3(i):
             za, zc = live["z", i]
-            zb = three.tile([P, M], F32, name="zb%d" % i, tag="zb")
+            zb = four.tile([P, M], F32, name="zb%d" % i, tag="zb")
             nc.vector.tensor_tensor(out=zb[:, 0:512], in0=za[:, 0:512], in1=bias[:, 0:512], op=ALU.add)
             nc.vector.tensor_tensor(out=zb[:, 512:896], in0=zc[:, 0:384], in1=bias[:, 512:896], op=ALU.add)
             live["zb", i] = zb
@@ -164,14 +164,6 @@ def tile_modelgraphpolicy_pb_t_kernel(tc, xum, action, up_w3, up_b3, dyn_w1_mu, 
             nc.gpsimd.tensor_tensor(out=rn[:, i : i + 1], in0=ssc[:, i : i + 1], in1=neghalf[:], op=ALU.pow)
 
         def scale(i):
-            if i % 3 == 1:
-                nc.scalar.activation(
-                    out=mu_all[:, i, :, 0:MSG],
-                    in_=live["zb", i][:].rearrange("p (u m) -> p u m", u=4),
-                    func=ACT.Copy,
-                    scale=rn[:, i : i + 1],
-                )
-                return
             nc.vector.tensor_scalar(
                 out=mu_all[:, i, :, 0:MSG],
                 in0=live["zb", i][:].rearrange("p (u m) -> p u m", u=4),
@@ -223,9 +215,7 @@ def tile_modelgraphpolicy_pb_t_kernel(tc, xum, action, up_w3, up_b3, dyn_w1_mu, 
 
         def relu_store(i):
             ot = live["ot", i // 2]
-            nc.gpsimd.tensor_scalar(
-                out=ot[:, i % 2, :], in0=ot[:, i % 2, :], scalar1=FMAX, scalar2=0.0, op0=ALU.min, op1=ALU.max
-            )
+            nc.scalar.activation(out=ot[:, i % 2, :], in_=ot[:, i % 2, :], func=ACT.Relu)
             if i >= NT - 2:
                 nc.sync.dma_start(out=o_v[:, i : i + 1, :], in_=ot[:, i % 2 : i % 2 + 1, :])
             elif i % 2 == 1:
@@ -263,10 +253,10 @@ def tile_modelgraphpolicy_pb_t_kernel(tc, xum, action, up_w3, up_b3, dyn_w1_mu, 
         tr_w3(3, ps_z, "z")
         ex_w3(0, nc.vector.tensor_copy)
         ex_w3(1, nc.scalar.copy)
-        ex_w3(2, nc.vector.tensor_copy)
-        ex_w3(3, nc.scalar.copy)
         q_x(0)
         quantise(w3g[:, 0:4, :, :].rearrange("p a n t -> p (a n t)"), w3c[:, 0:512], w3s[:, 0:512])
+        ex_w3(2, nc.vector.tensor_copy)
+        ex_w3(3, nc.scalar.copy)
         quantise(w3g[:, 4:6, :, :].rearrange("p a n t -> p (a n t)"), w3c[:, 512:768], w3s[:, 512:768])
         quantise(w3g[:, 6:7, :, :].rearrange("p a n t -> p (a n t)"), w3c[:, 768:896], w3s[:, 768:896])
         for b, (pool, tag, copy) in enumerate(
@@ -280,17 +270,14 @@ def tile_modelgraphpolicy_pb_t_kernel(tc, xum, action, up_w3, up_b3, dyn_w1_mu, 
         q_x(1)
         shuffle_action(mu_all, act_all, 0, 4)
 
-        LS = 3
-        LT, LE, L2, LB, LR = LS + 1, LS + 2, LS + 3, LS + 4, LS + 5
+        LQ2 = 2
+        LS = LQ2 + 2
+        LT, LE, LQ, L2, LB, LR = LS + 1, LS + 2, LS + 3, LS + 4, LS + 5, LS + 6
         for j in range(NT + LR + 1):
-            if 0 <= j - LR < NT:
-                relu_store(j - LR)
-            if 0 <= j - 2 < NT:
-                rnorm(j - 2)
-            if 3 <= j <= 9:
-                shuffle_action(mu_all, act_all, 4 * (j - 2), 4 * (j - 2) + 4)
             if 0 <= j - 1 < NT:
                 add_b3(j - 1)
+            if 0 <= j - LR < NT:
+                relu_store(j - LR)
             if 0 <= j - LB < NT:
                 add_b1(j - LB)
             if 0 <= j - LE < NT:
@@ -311,22 +298,25 @@ def tile_modelgraphpolicy_pb_t_kernel(tc, xum, action, up_w3, up_b3, dyn_w1_mu, 
                 stage1(j)
             if j % 2 == 1 and (j + 3) // 2 < NT // 2:
                 tr_x((j + 3) // 2)
-            if j == 2:
-                shuffle_action(w1p, w1a, 0, NW1)
             if j == 3:
                 tr_w1(0)
                 tr_w1(1)
             if j == 4:
                 tr_w1(2)
                 tr_w1(3)
+            if 0 <= j - LQ2 < NT:
+                squares(j - LQ2)
+                rnorm(j - LQ2)
+            if j == 2:
+                shuffle_action(w1p, w1a, 0, NW1)
+            if 3 <= j <= 9:
+                shuffle_action(mu_all, act_all, 4 * (j - 2), 4 * (j - 2) + 4)
             if 0 <= j - LS < NT:
                 scale(j - LS)
-            if 0 <= j - 1 < NT:
-                squares(j - 1)
-            if j % 2 == 0 and 2 <= (j + 2) // 2 < NT // 2:
-                q_x((j + 2) // 2)
+            if j % 2 == 1 and 2 <= (j + 1) // 2 < NT // 2:
+                q_x((j + 1) // 2)
             if j == 5:
                 for c in range(2):
                     quantise(w1g[:, c, :, :].rearrange("p f t -> p (f t)"), w1c[:, c, :], w1s[:, c, :])
-            if 0 <= j - LE < NT:
-                q_m(j - LE)
+            if 0 <= j - LQ < NT:
+                q_m(j - LQ)

@@ -30,7 +30,6 @@ def tile_modelgraphpolicy_pb_t_kernel(tc, xum, action, up_w3, up_b3, dyn_w1_mu, 
         keep = ctx.enter_context(tc.tile_pool(name="keep", bufs=1))
         two = ctx.enter_context(tc.tile_pool(name="two", bufs=2))
         three = ctx.enter_context(tc.tile_pool(name="three", bufs=3))
-        four = ctx.enter_context(tc.tile_pool(name="four", bufs=4))
         ps_z = ctx.enter_context(tc.psum_pool(name="ps_z", bufs=3))
         ps_t = ctx.enter_context(tc.psum_pool(name="ps_t", bufs=3))
         ps_o = ctx.enter_context(tc.psum_pool(name="ps_o", bufs=2))
@@ -58,6 +57,7 @@ def tile_modelgraphpolicy_pb_t_kernel(tc, xum, action, up_w3, up_b3, dyn_w1_mu, 
         ss = keep.tile([P, NT], F32, name="ss")
         ssc = keep.tile([P, NT], F32, name="ssc")
         rn = keep.tile([P, NT], F32, name="rn")
+        nrm = keep.tile([P, NT], F32, name="nrm")
 
         x_v = xum.rearrange("(p i) k -> p i k", i=NT)
         a_v = action.rearrange("(p i) a -> p i a", i=NT)
@@ -150,7 +150,7 @@ def tile_modelgraphpolicy_pb_t_kernel(tc, xum, action, up_w3, up_b3, dyn_w1_mu, 
 
         def add_b3(i):
             za, zc = live["z", i]
-            zb = four.tile([P, M], F32, name="zb%d" % i, tag="zb")
+            zb = three.tile([P, M], F32, name="zb%d" % i, tag="zb")
             nc.vector.tensor_tensor(out=zb[:, 0:512], in0=za[:, 0:512], in1=bias[:, 0:512], op=ALU.add)
             nc.vector.tensor_tensor(out=zb[:, 512:896], in0=zc[:, 0:384], in1=bias[:, 512:896], op=ALU.add)
             live["zb", i] = zb
@@ -159,17 +159,23 @@ def tile_modelgraphpolicy_pb_t_kernel(tc, xum, action, up_w3, up_b3, dyn_w1_mu, 
             junk = two.tile([P, M], BF16, name="junk%d" % i, tag="junk")
             nc.scalar.activation(out=junk[:], in_=live["zb", i][:], func=ACT.Square, accum_out=ss[:, i : i + 1])
 
-        def rnorm(i):
-            nc.gpsimd.tensor_scalar_max(out=ssc[:, i : i + 1], in0=ss[:, i : i + 1], scalar1=EPS2)
-            nc.gpsimd.tensor_tensor(out=rn[:, i : i + 1], in0=ssc[:, i : i + 1], in1=neghalf[:], op=ALU.pow)
+        def floor_ss(i):
+            nc.vector.tensor_scalar_max(out=ssc[:, i : i + 1], in0=ss[:, i : i + 1], scalar1=EPS2)
+
+        def root(i):
+            nc.scalar.activation(out=nrm[:, i : i + 1], in_=ssc[:, i : i + 1], func=ACT.Sqrt)
+
+        def recip(i):
+            nc.vector.reciprocal(out=rn[:, i : i + 1], in_=nrm[:, i : i + 1])
 
         def scale(i):
-            nc.vector.tensor_scalar(
+            nc.gpsimd.tensor_scalar(
                 out=mu_all[:, i, :, 0:MSG],
                 in0=live["zb", i][:].rearrange("p (u m) -> p u m", u=4),
                 scalar1=rn[:, i : i + 1],
-                scalar2=None,
+                scalar2=0.0,
                 op0=ALU.mult,
+                op1=ALU.add,
             )
 
         def tr_m(i):
@@ -215,7 +221,10 @@ def tile_modelgraphpolicy_pb_t_kernel(tc, xum, action, up_w3, up_b3, dyn_w1_mu, 
 
         def relu_store(i):
             ot = live["ot", i // 2]
-            nc.scalar.activation(out=ot[:, i % 2, :], in_=ot[:, i % 2, :], func=ACT.Relu)
+            if i % 2 == 0:
+                nc.vector.tensor_scalar_max(out=ot[:, i % 2, :], in0=ot[:, i % 2, :], scalar1=0.0)
+            else:
+                nc.scalar.activation(out=ot[:, i % 2, :], in_=ot[:, i % 2, :], func=ACT.Relu)
             if i >= NT - 2:
                 nc.sync.dma_start(out=o_v[:, i : i + 1, :], in_=ot[:, i % 2 : i % 2 + 1, :])
             elif i % 2 == 1:
@@ -223,7 +232,8 @@ def tile_modelgraphpolicy_pb_t_kernel(tc, xum, action, up_w3, up_b3, dyn_w1_mu, 
 
         nc.vector.memset(brow[:].bitcast(I32), 0)
         nc.vector.memset(ones[:], 1.0)
-        nc.vector.memset(neghalf[:], -0.5)
+        nc.vector.memset(neghalf[:], 1.0)
+        nc.scalar.activation(out=neghalf[:], in_=neghalf[:], func=ACT.Sqrt)
         make_identity(nc, ident[:])
 
         nc.sync.dma_start(out=x_all[:, 0:2, :], in_=x_v[:, 0:2, :])
@@ -270,20 +280,22 @@ def tile_modelgraphpolicy_pb_t_kernel(tc, xum, action, up_w3, up_b3, dyn_w1_mu, 
         q_x(1)
         shuffle_action(mu_all, act_all, 0, 4)
 
-        LQ2 = 2
-        LS = LQ2 + 2
-        LT, LE, LQ, L2, LB, LR = LS + 1, LS + 2, LS + 3, LS + 4, LS + 5, LS + 6
+        LT, LE, L2, LB, LR = 4, 5, 6, 7, 8
         for j in range(NT + LR + 1):
             if 0 <= j - 1 < NT:
                 add_b3(j - 1)
-            if 0 <= j - LR < NT:
-                relu_store(j - LR)
+            if 0 <= j - 2 < NT:
+                floor_ss(j - 2)
             if 0 <= j - LB < NT:
                 add_b1(j - LB)
+            if 0 <= j - LR < NT:
+                relu_store(j - LR)
             if 0 <= j - LE < NT:
                 ex_m(j - LE)
             if j % 2 == 0 and 2 <= (j + 2) // 2 < NT // 2:
                 ex_x((j + 2) // 2)
+            if 0 <= j - 2 < NT:
+                root(j - 2)
             if j == 4:
                 ex_w1(0, nc.scalar.copy)
                 ex_w1(1, nc.vector.tensor_copy)
@@ -304,19 +316,19 @@ def tile_modelgraphpolicy_pb_t_kernel(tc, xum, action, up_w3, up_b3, dyn_w1_mu, 
             if j == 4:
                 tr_w1(2)
                 tr_w1(3)
-            if 0 <= j - LQ2 < NT:
-                squares(j - LQ2)
-                rnorm(j - LQ2)
+            if 0 <= j - 1 < NT:
+                squares(j - 1)
+            if j % 2 == 0 and 2 <= (j + 2) // 2 < NT // 2:
+                q_x((j + 2) // 2)
+            if j == 5:
+                for c in range(2):
+                    quantise(w1g[:, c, :, :].rearrange("p f t -> p (f t)"), w1c[:, c, :], w1s[:, c, :])
+            if 0 <= j - LE < NT:
+                q_m(j - LE)
+            if 0 <= j - 2 < NT:
+                recip(j - 2)
+                scale(j - 2)
             if j == 2:
                 shuffle_action(w1p, w1a, 0, NW1)
             if 3 <= j <= 9:
                 shuffle_action(mu_all, act_all, 4 * (j - 2), 4 * (j - 2) + 4)
-            if 0 <= j - LS < NT:
-                scale(j - LS)
-            if j % 2 == 1 and 2 <= (j + 1) // 2 < NT // 2:
-                q_x((j + 1) // 2)
-            if j == 5:
-                for c in range(2):
-                    quantise(w1g[:, c, :, :].rearrange("p f t -> p (f t)"), w1c[:, c, :], w1s[:, c, :])
-            if 0 <= j - LQ < NT:
-                q_m(j - LQ)

@@ -19,7 +19,7 @@ NW3 = M // P
 NW1 = F1 // P
 MSG = 224
 ACO = 32
-EPS2 = 1e-24
+RMAX = 1e12
 
 FLOPS = 2 * B * H * M + 2 * B * (M + A) * F1
 
@@ -55,7 +55,6 @@ def tile_modelgraphpolicy_pb_t_kernel(tc, xum, action, up_w3, up_b3, dyn_w1_mu, 
         xc = keep.tile([P, NT, P], U32, name="xc", align_bytes=64)
         xs = keep.tile([P, NT, P], U8, name="xs", align_bytes=64)
         ss = keep.tile([P, NT], F32, name="ss")
-        ssc = keep.tile([P, NT], F32, name="ssc")
         rn = keep.tile([P, NT], F32, name="rn")
         nrm = keep.tile([P, NT], F32, name="nrm")
 
@@ -159,14 +158,11 @@ def tile_modelgraphpolicy_pb_t_kernel(tc, xum, action, up_w3, up_b3, dyn_w1_mu, 
             junk = two.tile([P, M], BF16, name="junk%d" % i, tag="junk")
             nc.scalar.activation(out=junk[:], in_=live["zb", i][:], func=ACT.Square, accum_out=ss[:, i : i + 1])
 
-        def floor_ss(i):
-            nc.vector.tensor_scalar_max(out=ssc[:, i : i + 1], in0=ss[:, i : i + 1], scalar1=EPS2)
-
         def root(i):
-            nc.scalar.activation(out=nrm[:, i : i + 1], in_=ssc[:, i : i + 1], func=ACT.Sqrt)
+            nc.scalar.activation(out=nrm[:, i : i + 1], in_=ss[:, i : i + 1], func=ACT.Abs_reciprocal_sqrt)
 
         def recip(i):
-            nc.vector.reciprocal(out=rn[:, i : i + 1], in_=nrm[:, i : i + 1])
+            nc.vector.tensor_scalar_min(out=rn[:, i : i + 1], in0=nrm[:, i : i + 1], scalar1=RMAX)
 
         def scale(i):
             nc.gpsimd.tensor_scalar(
@@ -221,7 +217,7 @@ def tile_modelgraphpolicy_pb_t_kernel(tc, xum, action, up_w3, up_b3, dyn_w1_mu, 
 
         def relu_store(i):
             ot = live["ot", i // 2]
-            if i % 2 == 0:
+            if i % 2 == 1:
                 nc.vector.tensor_scalar_max(out=ot[:, i % 2, :], in0=ot[:, i % 2, :], scalar1=0.0)
             else:
                 nc.scalar.activation(out=ot[:, i % 2, :], in_=ot[:, i % 2, :], func=ACT.Relu)
@@ -233,7 +229,7 @@ def tile_modelgraphpolicy_pb_t_kernel(tc, xum, action, up_w3, up_b3, dyn_w1_mu, 
         nc.vector.memset(brow[:].bitcast(I32), 0)
         nc.vector.memset(ones[:], 1.0)
         nc.vector.memset(neghalf[:], 1.0)
-        nc.scalar.activation(out=neghalf[:], in_=neghalf[:], func=ACT.Sqrt)
+        nc.scalar.activation(out=neghalf[:], in_=neghalf[:], func=ACT.Abs_reciprocal_sqrt)
         make_identity(nc, ident[:])
 
         nc.sync.dma_start(out=x_all[:, 0:2, :], in_=x_v[:, 0:2, :])
@@ -284,18 +280,16 @@ def tile_modelgraphpolicy_pb_t_kernel(tc, xum, action, up_w3, up_b3, dyn_w1_mu, 
         for j in range(NT + LR + 1):
             if 0 <= j - 1 < NT:
                 add_b3(j - 1)
-            if 0 <= j - 2 < NT:
-                floor_ss(j - 2)
             if 0 <= j - LB < NT:
                 add_b1(j - LB)
-            if 0 <= j - LR < NT:
-                relu_store(j - LR)
             if 0 <= j - LE < NT:
                 ex_m(j - LE)
-            if j % 2 == 0 and 2 <= (j + 2) // 2 < NT // 2:
-                ex_x((j + 2) // 2)
             if 0 <= j - 2 < NT:
                 root(j - 2)
+            if 0 <= j - LR < NT:
+                relu_store(j - LR)
+            if j % 2 == 0 and 2 <= (j + 2) // 2 < NT // 2:
+                ex_x((j + 2) // 2)
             if j == 4:
                 ex_w1(0, nc.scalar.copy)
                 ex_w1(1, nc.vector.tensor_copy)

@@ -217,7 +217,7 @@ def tile_modelgraphpolicy_pb_t_kernel(tc, xum, action, up_w3, up_b3, dyn_w1_mu, 
 
         def relu_store(i):
             ot = live["ot", i // 2]
-            if i % 2 == 1:
+            if i % 2 == 0:
                 nc.vector.tensor_scalar_max(out=ot[:, i % 2, :], in0=ot[:, i % 2, :], scalar1=0.0)
             else:
                 nc.scalar.activation(out=ot[:, i % 2, :], in_=ot[:, i % 2, :], func=ACT.Relu)
@@ -312,8 +312,8 @@ def tile_modelgraphpolicy_pb_t_kernel(tc, xum, action, up_w3, up_b3, dyn_w1_mu, 
                 tr_w1(3)
             if 0 <= j - 1 < NT:
                 squares(j - 1)
-            if j % 2 == 0 and 2 <= (j + 2) // 2 < NT // 2:
-                q_x((j + 2) // 2)
+            if j % 2 == 1 and 2 <= (j + 1) // 2 < NT // 2:
+                q_x((j + 1) // 2)
             if j == 5:
                 for c in range(2):
                     quantise(w1g[:, c, :, :].rearrange("p f t -> p (f t)"), w1c[:, c, :], w1s[:, c, :])

@@ -15,11 +15,13 @@ ACT = mybir.ActivationFunctionType
 P = 128
 B, H, A, M, F1 = 4096, 512, 128, 896, 512
 NT = B // P
+NP = NT // 2
 NW3 = M // P
 NW1 = F1 // P
 MSG = 224
 ACO = 32
 RMAX = 1e12
+FMAX = 3.4028234663852886e38
 
 FLOPS = 2 * B * H * M + 2 * B * (M + A) * F1
 
@@ -29,7 +31,7 @@ def tile_modelgraphpolicy_pb_t_kernel(tc, xum, action, up_w3, up_b3, dyn_w1_mu, 
     with ExitStack() as ctx:
         keep = ctx.enter_context(tc.tile_pool(name="keep", bufs=1))
         two = ctx.enter_context(tc.tile_pool(name="two", bufs=2))
-        three = ctx.enter_context(tc.tile_pool(name="three", bufs=3))
+        four = ctx.enter_context(tc.tile_pool(name="four", bufs=4))
         ps_z = ctx.enter_context(tc.psum_pool(name="ps_z", bufs=3))
         ps_t = ctx.enter_context(tc.psum_pool(name="ps_t", bufs=3))
         ps_o = ctx.enter_context(tc.psum_pool(name="ps_o", bufs=2))
@@ -39,7 +41,7 @@ def tile_modelgraphpolicy_pb_t_kernel(tc, xum, action, up_w3, up_b3, dyn_w1_mu, 
         ones = keep.tile([P, P], BF16, name="ones")
         brow = keep.tile([P, 3 * 512], BF16, name="brow")
         bias = keep.tile([P, 3 * 512], F32, name="bias")
-        neghalf = keep.tile([P, 1], F32, name="neghalf")
+        warm = keep.tile([P, 1], F32, name="warm")
         x_all = keep.tile([P, NT, H], BF16, name="x_all")
         act_all = keep.tile([P, NT, A], BF16, name="act_all")
         w3_raw = keep.tile([P, NW3, H], BF16, name="w3_raw")
@@ -55,8 +57,8 @@ def tile_modelgraphpolicy_pb_t_kernel(tc, xum, action, up_w3, up_b3, dyn_w1_mu, 
         xc = keep.tile([P, NT, P], U32, name="xc", align_bytes=64)
         xs = keep.tile([P, NT, P], U8, name="xs", align_bytes=64)
         ss = keep.tile([P, NT], F32, name="ss")
-        rn = keep.tile([P, NT], F32, name="rn")
         nrm = keep.tile([P, NT], F32, name="nrm")
+        rn = keep.tile([P, NT], F32, name="rn")
 
         x_v = xum.rearrange("(p i) k -> p i k", i=NT)
         a_v = action.rearrange("(p i) a -> p i a", i=NT)
@@ -132,37 +134,49 @@ def tile_modelgraphpolicy_pb_t_kernel(tc, xum, action, up_w3, up_b3, dyn_w1_mu, 
         def ex_w1(r, copy):
             leave_bank(copy, w1g[:, :, P * r : P * r + P, :], live["tw1", r], 2)
 
-        def stage1(i):
-            za = ps_z.tile([P, 512], F32, name="za%d" % i, tag="z")
-            zc = ps_z.tile([P, 512], F32, name="zc%d" % i, tag="z")
-            for dst, lo, hi in ((za[:, 0:512], 0, 512), (zc[:, 0:256], 512, 768), (zc[:, 256:384], 768, 896)):
-                nc.tensor.matmul_mx(
-                    out=dst,
-                    lhsT=xc[:, i, :].bitcast(FP8X4),
-                    lhsT_scale=xs[:, i, :],
-                    rhs=w3c[:, lo:hi].bitcast(FP8X4),
-                    rhs_scale=w3s[:, lo:hi],
-                    start=True,
-                    stop=True,
-                )
-            live["z", i] = (za, zc)
+        def z_pass(i, dst, lo, hi):
+            nc.tensor.matmul_mx(
+                out=dst,
+                lhsT=xc[:, i, :].bitcast(FP8X4),
+                lhsT_scale=xs[:, i, :],
+                rhs=w3c[:, lo:hi].bitcast(FP8X4),
+                rhs_scale=w3s[:, lo:hi],
+                start=True,
+                stop=True,
+            )
+
+        def z_lo(i):
+            live["za", i] = za = ps_z.tile([P, 512], F32, name="za%d" % i, tag="z")
+            z_pass(i, za[:, 0:512], 0, 512)
+
+        def z_hi(i):
+            live["zc", i] = zc = ps_z.tile([P, 512], F32, name="zc%d" % i, tag="z")
+            z_pass(i, zc[:, 0:256], 512, 768)
+            z_pass(i, zc[:, 256:384], 768, 896)
 
         def add_b3(i):
-            za, zc = live["z", i]
-            zb = three.tile([P, M], F32, name="zb%d" % i, tag="zb")
-            nc.vector.tensor_tensor(out=zb[:, 0:512], in0=za[:, 0:512], in1=bias[:, 0:512], op=ALU.add)
-            nc.vector.tensor_tensor(out=zb[:, 512:896], in0=zc[:, 0:384], in1=bias[:, 512:896], op=ALU.add)
-            live["zb", i] = zb
+            live["zb", i] = zb = four.tile([P, M], F32, name="zb%d" % i, tag="zb")
+            nc.vector.tensor_tensor(out=zb[:, 0:512], in0=live["za", i][:], in1=bias[:, 0:512], op=ALU.add)
+            nc.vector.tensor_tensor(out=zb[:, 512:896], in0=live["zc", i][:, 0:384], in1=bias[:, 512:896], op=ALU.add)
 
         def squares(i):
             junk = two.tile([P, M], BF16, name="junk%d" % i, tag="junk")
             nc.scalar.activation(out=junk[:], in_=live["zb", i][:], func=ACT.Square, accum_out=ss[:, i : i + 1])
 
-        def root(i):
-            nc.scalar.activation(out=nrm[:, i : i + 1], in_=ss[:, i : i + 1], func=ACT.Abs_reciprocal_sqrt)
+        def root(k):
+            nc.scalar.activation(
+                out=nrm[:, 2 * k : 2 * k + 2], in_=ss[:, 2 * k : 2 * k + 2], func=ACT.Abs_reciprocal_sqrt
+            )
 
-        def recip(i):
-            nc.vector.tensor_scalar_min(out=rn[:, i : i + 1], in0=nrm[:, i : i + 1], scalar1=RMAX)
+        def norm_factor(k):
+            nc.gpsimd.tensor_scalar(
+                out=rn[:, 2 * k : 2 * k + 2],
+                in0=nrm[:, 2 * k : 2 * k + 2],
+                scalar1=RMAX,
+                scalar2=0.0,
+                op0=ALU.min,
+                op1=ALU.max,
+            )
 
         def scale(i):
             nc.gpsimd.tensor_scalar(
@@ -174,62 +188,91 @@ def tile_modelgraphpolicy_pb_t_kernel(tc, xum, action, up_w3, up_b3, dyn_w1_mu, 
                 op1=ALU.add,
             )
 
+        def normalise(k):
+            norm_factor(k)
+            scale(2 * k)
+            if k < NP - 1:
+                scale(2 * k + 1)
+            else:
+                nc.scalar.activation(
+                    out=mu_all[:, 2 * k + 1, :, 0:MSG],
+                    in_=live["zb", 2 * k + 1][:].rearrange("p (u m) -> p u m", u=4),
+                    func=ACT.Copy,
+                    scale=rn[:, 2 * k + 1 : 2 * k + 2],
+                )
+
         def tr_m(i):
             bank = ps_t.tile([P, 4, P], F32, name="tm%d" % i, tag="t")
             transpose_words(bank, [mu_all[:, i, u, :].bitcast(F32) for u in range(4)])
             live["tm", i] = bank
 
-        def ex_m(i):
-            mug = two.tile([P, 2, P, 4], BF16, name="mug%d" % i, tag="mug", align_bytes=64)
-            leave_bank(nc.scalar.copy, mug[:], live["tm", i], 2)
-            live["mug", i] = mug
+        def ex_m(k):
+            live["mug", k] = mug = two.tile([P, 2, 2, P, 4], BF16, name="mug%d" % k, tag="mug", align_bytes=64)
+            for a in range(2):
+                leave_bank(nc.scalar.copy, mug[:, a, :, :, :], live["tm", 2 * k + a], 2)
 
-        def q_m(i):
-            muc = three.tile([P, 2, P], U32, name="muc%d" % i, tag="muc", align_bytes=64)
-            mus = three.tile([P, 2, P], U8, name="mus%d" % i, tag="mus", align_bytes=64)
-            quantise(
-                live["mug", i][:].rearrange("p c n t -> p (c n t)"),
-                muc[:].rearrange("p c n -> p (c n)"),
-                mus[:].rearrange("p c n -> p (c n)"),
-            )
-            live["muc", i] = (muc, mus)
+        def q_m(k):
+            live["muc", k] = muc = two.tile([P, 2, 2, P], U32, name="muc%d" % k, tag="muc", align_bytes=64)
+            live["mus", k] = mus = two.tile([P, 2, 2, P], U8, name="mus%d" % k, tag="mus", align_bytes=64)
+            mug = live["mug", k]
+            if k < NP - 1:
+                quantise(
+                    mug[:].rearrange("p a c n t -> p (a c n t)"),
+                    muc[:].rearrange("p a c n -> p (a c n)"),
+                    mus[:].rearrange("p a c n -> p (a c n)"),
+                )
+            else:
+                for a in range(2):
+                    quantise(
+                        mug[:, a, :, :, :].rearrange("p c n t -> p (c n t)"),
+                        muc[:, a, :, :].rearrange("p c n -> p (c n)"),
+                        mus[:, a, :, :].rearrange("p c n -> p (c n)"),
+                    )
 
         def stage2(i):
-            muc, mus = live["muc", i]
-            acc = ps_o.tile([P, F1], F32, name="acc%d" % i, tag="o")
+            k, a = divmod(i, 2)
+            pool, tag = (ps_o, "o") if k < NP - 1 else (ps_z, "z")
+            live["acc", i] = acc = pool.tile([P, F1], F32, name="acc%d" % i, tag=tag)
             for c in range(2):
                 nc.tensor.matmul_mx(
                     out=acc[:],
-                    lhsT=muc[:, c, :].bitcast(FP8X4),
-                    lhsT_scale=mus[:, c, :],
+                    lhsT=live["muc", k][:, a, c, :].bitcast(FP8X4),
+                    lhsT_scale=live["mus", k][:, a, c, :],
                     rhs=w1c[:, c, :].bitcast(FP8X4),
                     rhs_scale=w1s[:, c, :],
                     start=(c == 0),
                     stop=(c == 1),
                 )
-            live["acc", i] = acc
 
         def add_b1(i):
-            if i % 2 == 0:
-                live["ot", i // 2] = three.tile([P, 2, F1], F32, name="ot%d" % (i // 2), tag="ot")
-            ot = live["ot", i // 2]
-            nc.vector.tensor_tensor(out=ot[:, i % 2, :], in0=live["acc", i][:], in1=bias[:, 1024:1536], op=ALU.add)
+            k, a = divmod(i, 2)
+            if a == 0:
+                live["ot", k] = four.tile([P, 2, F1], F32, name="ot%d" % k, tag="ot")
+            nc.vector.tensor_tensor(
+                out=live["ot", k][:, a, :], in0=live["acc", i][:], in1=bias[:, 1024:1536], op=ALU.add
+            )
 
-        def relu_store(i):
-            ot = live["ot", i // 2]
-            if i % 2 == 0:
-                nc.vector.tensor_scalar_max(out=ot[:, i % 2, :], in0=ot[:, i % 2, :], scalar1=0.0)
-            else:
-                nc.scalar.activation(out=ot[:, i % 2, :], in_=ot[:, i % 2, :], func=ACT.Relu)
-            if i >= NT - 2:
-                nc.sync.dma_start(out=o_v[:, i : i + 1, :], in_=ot[:, i % 2 : i % 2 + 1, :])
-            elif i % 2 == 1:
-                nc.sync.dma_start(out=o_v[:, i - 1 : i + 1, :], in_=ot[:])
+        def relu_g(k):
+            ot = live["ot", k]
+            nc.gpsimd.tensor_scalar(
+                out=ot[:, 1, :], in0=ot[:, 1, :], scalar1=FMAX, scalar2=0.0, op0=ALU.min, op1=ALU.max
+            )
+
+        def relu_s(k, a, lo, hi):
+            ot = live["ot", k]
+            nc.scalar.activation(out=ot[:, a, lo:hi], in_=ot[:, a, lo:hi], func=ACT.Relu)
+
+        def relu_v(k, a, lo, hi):
+            ot = live["ot", k]
+            nc.vector.tensor_scalar_max(out=ot[:, a, lo:hi], in0=ot[:, a, lo:hi], scalar1=0.0)
+
+        def store(k, lo, hi):
+            nc.sync.dma_start(out=o_v[:, 2 * k + lo : 2 * k + hi, :], in_=live["ot", k][:, lo:hi, :])
 
         nc.vector.memset(brow[:].bitcast(I32), 0)
         nc.vector.memset(ones[:], 1.0)
-        nc.vector.memset(neghalf[:], 1.0)
-        nc.scalar.activation(out=neghalf[:], in_=neghalf[:], func=ACT.Abs_reciprocal_sqrt)
+        nc.vector.memset(warm[:], 1.0)
+        nc.scalar.activation(out=warm[:], in_=warm[:], func=ACT.Abs_reciprocal_sqrt)
         make_identity(nc, ident[:])
 
         nc.sync.dma_start(out=x_all[:, 0:2, :], in_=x_v[:, 0:2, :])
@@ -257,6 +300,7 @@ def tile_modelgraphpolicy_pb_t_kernel(tc, xum, action, up_w3, up_b3, dyn_w1_mu, 
         tr_w3(1, ps_t, "t")
         tr_w3(2, ps_z, "z")
         tr_w3(3, ps_z, "z")
+        tr_x(1)
         ex_w3(0, nc.vector.tensor_copy)
         ex_w3(1, nc.scalar.copy)
         q_x(0)
@@ -265,64 +309,86 @@ def tile_modelgraphpolicy_pb_t_kernel(tc, xum, action, up_w3, up_b3, dyn_w1_mu, 
         ex_w3(3, nc.scalar.copy)
         quantise(w3g[:, 4:6, :, :].rearrange("p a n t -> p (a n t)"), w3c[:, 512:768], w3s[:, 512:768])
         quantise(w3g[:, 6:7, :, :].rearrange("p a n t -> p (a n t)"), w3c[:, 768:896], w3s[:, 768:896])
+        ex_x(1)
         for b, (pool, tag, copy) in enumerate(
             ((ps_z, "z", nc.vector.tensor_copy), (ps_o, "o", nc.scalar.copy), (ps_o, "o", nc.scalar.copy))
         ):
             spread = pool.tile([P, 512], F32, name="spread%d" % b, tag=tag)
             nc.tensor.matmul(out=spread[:], lhsT=ones[:], rhs=brow[:, 512 * b : 512 * b + 512], start=True, stop=True)
             copy(out=bias[:, 512 * b : 512 * b + 512], in_=spread[:])
-        tr_x(1)
-        ex_x(1)
+        z_lo(0)
+        z_hi(0)
+        z_lo(1)
         q_x(1)
+        tr_x(2)
         shuffle_action(mu_all, act_all, 0, 4)
+        shuffle_action(w1p, w1a, 0, NW1)
 
-        LT, LE, L2, LB, LR = 4, 5, 6, 7, 8
-        for j in range(NT + LR + 1):
-            if 0 <= j - 1 < NT:
-                add_b3(j - 1)
-            if 0 <= j - LB < NT:
-                add_b1(j - LB)
-            if 0 <= j - LE < NT:
-                ex_m(j - LE)
-            if 0 <= j - 2 < NT:
-                root(j - 2)
-            if 0 <= j - LR < NT:
-                relu_store(j - LR)
-            if j % 2 == 0 and 2 <= (j + 2) // 2 < NT // 2:
-                ex_x((j + 2) // 2)
-            if j == 4:
-                ex_w1(0, nc.scalar.copy)
-                ex_w1(1, nc.vector.tensor_copy)
-            if j == 5:
-                ex_w1(2, nc.scalar.copy)
-                ex_w1(3, nc.vector.tensor_copy)
-            if 0 <= j - LT < NT:
-                tr_m(j - LT)
-            if 0 <= j - L2 < NT:
-                stage2(j - L2)
-            if j < NT:
-                stage1(j)
-            if j % 2 == 1 and (j + 3) // 2 < NT // 2:
-                tr_x((j + 3) // 2)
-            if j == 3:
-                tr_w1(0)
-                tr_w1(1)
-            if j == 4:
-                tr_w1(2)
-                tr_w1(3)
-            if 0 <= j - 1 < NT:
-                squares(j - 1)
-            if j % 2 == 1 and 2 <= (j + 1) // 2 < NT // 2:
-                q_x((j + 1) // 2)
-            if j == 5:
+        def there(k):
+            return 0 <= k < NP
+
+        for k in range(NP + 3):
+            if there(k):
+                add_b3(2 * k)
+            if there(k - 3):
+                stage2(2 * k - 6)
+                stage2(2 * k - 5)
+            if there(k):
+                z_hi(2 * k + 1)
+                add_b3(2 * k + 1)
+            if 1 <= k <= 2:
+                ex_w1(2 * k - 2, nc.vector.tensor_copy)
+            if k == NP + 1:
+                ex_m(k - 2)
+                q_m(k - 2)
+            if there(k - 3):
+                add_b1(2 * k - 6)
+                add_b1(2 * k - 5)
+            if there(k - 1) and k == NP:
+                normalise(k - 1)
+            if there(k - 2) and k <= NP:
+                ex_m(k - 2)
+            if there(k):
+                squares(2 * k)
+            if there(k + 2):
+                ex_x(k + 2)
+            if 1 <= k <= 2:
+                ex_w1(2 * k - 1, nc.scalar.copy)
+            if there(k):
+                squares(2 * k + 1)
+            if there(k - 1) and k < NP:
+                normalise(k - 1)
+            if there(k - 4) and k - 4 < NP - 1:
+                relu_g(k - 4)
+            if there(k + 1):
+                z_lo(2 * k + 2)
+                z_hi(2 * k + 2)
+                z_lo(2 * k + 3)
+            if there(k - 1):
+                tr_m(2 * k - 2)
+                tr_m(2 * k - 1)
+            if there(k + 3):
+                tr_x(k + 3)
+            if k < 2:
+                tr_w1(2 * k)
+                tr_w1(2 * k + 1)
+            if there(k - 2) and k <= NP:
+                q_m(k - 2)
+            if there(k + 2):
+                q_x(k + 2)
+            if k == 2:
                 for c in range(2):
                     quantise(w1g[:, c, :, :].rearrange("p f t -> p (f t)"), w1c[:, c, :], w1s[:, c, :])
-            if 0 <= j - LE < NT:
-                q_m(j - LE)
-            if 0 <= j - 2 < NT:
-                recip(j - 2)
-                scale(j - 2)
-            if j == 2:
-                shuffle_action(w1p, w1a, 0, NW1)
-            if 3 <= j <= 9:
-                shuffle_action(mu_all, act_all, 4 * (j - 2), 4 * (j - 2) + 4)
+            if there(k):
+                root(k)
+            if there(k - 4) and k - 4 < NP - 1:
+                relu_s(k - 4, 0, 0, F1 // 2)
+                relu_v(k - 4, 0, F1 // 2, F1)
+                store(k - 4, 0, 2)
+            if k - 3 == NP - 1:
+                relu_s(k - 3, 0, 0, F1)
+                store(k - 3, 0, 1)
+                relu_v(k - 3, 1, 0, F1)
+                store(k - 3, 1, 2)
+            if k < 4:
+                shuffle_action(mu_all, act_all, 4 + 7 * k, 11 + 7 * k)

@@ -21,7 +21,6 @@ NW1 = F1 // P
 MSG = 224
 ACO = 32
 RMAX = 1e12
-FMAX = 3.4028234663852886e38
 
 FLOPS = 2 * B * H * M + 2 * B * (M + A) * F1
 
@@ -169,14 +168,7 @@ def tile_modelgraphpolicy_pb_t_kernel(tc, xum, action, up_w3, up_b3, dyn_w1_mu, 
             )
 
         def norm_factor(k):
-            nc.gpsimd.tensor_scalar(
-                out=rn[:, 2 * k : 2 * k + 2],
-                in0=nrm[:, 2 * k : 2 * k + 2],
-                scalar1=RMAX,
-                scalar2=0.0,
-                op0=ALU.min,
-                op1=ALU.max,
-            )
+            nc.vector.tensor_scalar_min(out=rn[:, 2 * k : 2 * k + 2], in0=nrm[:, 2 * k : 2 * k + 2], scalar1=RMAX)
 
         def scale(i):
             nc.gpsimd.tensor_scalar(
@@ -189,7 +181,6 @@ def tile_modelgraphpolicy_pb_t_kernel(tc, xum, action, up_w3, up_b3, dyn_w1_mu, 
             )
 
         def normalise(k):
-            norm_factor(k)
             scale(2 * k)
             if k < NP - 1:
                 scale(2 * k + 1)
@@ -252,19 +243,13 @@ def tile_modelgraphpolicy_pb_t_kernel(tc, xum, action, up_w3, up_b3, dyn_w1_mu, 
                 out=live["ot", k][:, a, :], in0=live["acc", i][:], in1=bias[:, 1024:1536], op=ALU.add
             )
 
-        def relu_g(k):
+        def relu_s(k, a):
             ot = live["ot", k]
-            nc.gpsimd.tensor_scalar(
-                out=ot[:, 1, :], in0=ot[:, 1, :], scalar1=FMAX, scalar2=0.0, op0=ALU.min, op1=ALU.max
-            )
+            nc.scalar.activation(out=ot[:, a, :], in_=ot[:, a, :], func=ACT.Relu)
 
-        def relu_s(k, a, lo, hi):
+        def relu_v(k, a):
             ot = live["ot", k]
-            nc.scalar.activation(out=ot[:, a, lo:hi], in_=ot[:, a, lo:hi], func=ACT.Relu)
-
-        def relu_v(k, a, lo, hi):
-            ot = live["ot", k]
-            nc.vector.tensor_scalar_max(out=ot[:, a, lo:hi], in0=ot[:, a, lo:hi], scalar1=0.0)
+            nc.vector.tensor_scalar_max(out=ot[:, a, :], in0=ot[:, a, :], scalar1=0.0)
 
         def store(k, lo, hi):
             nc.sync.dma_start(out=o_v[:, 2 * k + lo : 2 * k + hi, :], in_=live["ot", k][:, lo:hi, :])
@@ -328,6 +313,8 @@ def tile_modelgraphpolicy_pb_t_kernel(tc, xum, action, up_w3, up_b3, dyn_w1_mu, 
             return 0 <= k < NP
 
         for k in range(NP + 3):
+            if there(k - 1):
+                norm_factor(k - 1)
             if there(k):
                 add_b3(2 * k)
             if there(k - 3):
@@ -358,8 +345,6 @@ def tile_modelgraphpolicy_pb_t_kernel(tc, xum, action, up_w3, up_b3, dyn_w1_mu, 
                 squares(2 * k + 1)
             if there(k - 1) and k < NP:
                 normalise(k - 1)
-            if there(k - 4) and k - 4 < NP - 1:
-                relu_g(k - 4)
             if there(k + 1):
                 z_lo(2 * k + 2)
                 z_hi(2 * k + 2)
@@ -382,13 +367,13 @@ def tile_modelgraphpolicy_pb_t_kernel(tc, xum, action, up_w3, up_b3, dyn_w1_mu, 
             if there(k):
                 root(k)
             if there(k - 4) and k - 4 < NP - 1:
-                relu_s(k - 4, 0, 0, F1 // 2)
-                relu_v(k - 4, 0, F1 // 2, F1)
+                relu_v(k - 4, 0)
+                relu_s(k - 4, 1)
                 store(k - 4, 0, 2)
             if k - 3 == NP - 1:
-                relu_s(k - 3, 0, 0, F1)
+                relu_s(k - 3, 0)
                 store(k - 3, 0, 1)
-                relu_v(k - 3, 1, 0, F1)
+                relu_v(k - 3, 1)
                 store(k - 3, 1, 2)
             if k < 4:
                 shuffle_action(mu_all, act_all, 4 + 7 * k, 11 + 7 * k)

@@ -31,15 +31,17 @@ def tile_modelgraphpolicy_pb_t_kernel(tc, xum, action, up_w3, up_b3, dyn_w1_mu, 
         keep = ctx.enter_context(tc.tile_pool(name="keep", bufs=1))
         two = ctx.enter_context(tc.tile_pool(name="two", bufs=2))
         four = ctx.enter_context(tc.tile_pool(name="four", bufs=4))
-        ps_z = ctx.enter_context(tc.psum_pool(name="ps_z", bufs=3))
-        ps_t = ctx.enter_context(tc.psum_pool(name="ps_t", bufs=3))
+        six = ctx.enter_context(tc.tile_pool(name="six", bufs=6))
+        ps_z = ctx.enter_context(tc.psum_pool(name="ps_z", bufs=4))
+        ps_t = ctx.enter_context(tc.psum_pool(name="ps_t", bufs=2))
         ps_o = ctx.enter_context(tc.psum_pool(name="ps_o", bufs=2))
         ctx.enter_context(tc.manual_schedule())
 
         ident = keep.tile([P, P], F32, name="ident")
         ones = keep.tile([P, P], BF16, name="ones")
-        brow = keep.tile([P, 3 * 512], BF16, name="brow")
-        bias = keep.tile([P, 3 * 512], F32, name="bias")
+        brow3 = keep.tile([P, M], BF16, name="brow3")
+        bias3 = keep.tile([P, M], F32, name="bias3")
+        bias1 = keep.tile([P, F1], BF16, name="bias1")
         warm = keep.tile([P, 1], F32, name="warm")
         x_all = keep.tile([P, NT, H], BF16, name="x_all")
         act_all = keep.tile([P, NT, A], BF16, name="act_all")
@@ -79,11 +81,11 @@ def tile_modelgraphpolicy_pb_t_kernel(tc, xum, action, up_w3, up_b3, dyn_w1_mu, 
         def quantise(grouped, codes, scales):
             nc.vector.quantize_mx(out=codes.bitcast(FP8X4), scales=scales, in_=grouped)
 
-        def shuffle_action(dst4, src, lo, hi):
+        def shuffle_action(engine, dst4, src, lo, hi):
             dst = dst4[:].rearrange("p i (c h) m -> p (i c) h m", h=2)
             srv = src[:].rearrange("p i (c g h j) -> p (i c) g h j", c=2, g=2, h=2)
             for h in range(2):
-                nc.gpsimd.tensor_scalar(
+                engine.tensor_scalar(
                     out=dst[:, 2 * lo : 2 * hi, h, MSG : MSG + ACO].rearrange("p a (g j) -> p a g j", g=2),
                     in0=srv[:, 2 * lo : 2 * hi, :, h, :],
                     scalar1=1.0,
@@ -125,6 +127,12 @@ def tile_modelgraphpolicy_pb_t_kernel(tc, xum, action, up_w3, up_b3, dyn_w1_mu, 
             n = min(2, NW3 - 2 * k)
             leave_bank(copy, w3g[:, 2 * k : 2 * k + n, :, :], live["tw3", k], n)
 
+        def spread(row, wide, copy):
+            bank = ps_o.tile([P, 512], F32, name="spread", tag="o")
+            n = row.shape[1]
+            nc.tensor.matmul(out=bank[:, 0:n], lhsT=ones[:], rhs=row, start=True, stop=True)
+            copy(out=wide, in_=bank[:, 0:n])
+
         def tr_w1(r):
             bank = ps_o.tile([P, 4, P], F32, name="tw1%d" % r, tag="o")
             transpose_words(bank, [w1p[:, r, u, :].bitcast(F32) for u in range(4)])
@@ -154,9 +162,9 @@ def tile_modelgraphpolicy_pb_t_kernel(tc, xum, action, up_w3, up_b3, dyn_w1_mu, 
             z_pass(i, zc[:, 256:384], 768, 896)
 
         def add_b3(i):
-            live["zb", i] = zb = four.tile([P, M], F32, name="zb%d" % i, tag="zb")
-            nc.vector.tensor_tensor(out=zb[:, 0:512], in0=live["za", i][:], in1=bias[:, 0:512], op=ALU.add)
-            nc.vector.tensor_tensor(out=zb[:, 512:896], in0=live["zc", i][:, 0:384], in1=bias[:, 512:896], op=ALU.add)
+            live["zb", i] = zb = six.tile([P, M], F32, name="zb%d" % i, tag="zb")
+            nc.vector.tensor_tensor(out=zb[:, 0:512], in0=live["za", i][:], in1=bias3[:, 0:512], op=ALU.add)
+            nc.vector.tensor_tensor(out=zb[:, 512:896], in0=live["zc", i][:, 0:384], in1=bias3[:, 512:896], op=ALU.add)
 
         def squares(i):
             junk = two.tile([P, M], BF16, name="junk%d" % i, tag="junk")
@@ -170,8 +178,8 @@ def tile_modelgraphpolicy_pb_t_kernel(tc, xum, action, up_w3, up_b3, dyn_w1_mu, 
         def norm_factor(k):
             nc.vector.tensor_scalar_min(out=rn[:, 2 * k : 2 * k + 2], in0=nrm[:, 2 * k : 2 * k + 2], scalar1=RMAX)
 
-        def scale(i):
-            nc.gpsimd.tensor_scalar(
+        def scale(i, engine):
+            engine.tensor_scalar(
                 out=mu_all[:, i, :, 0:MSG],
                 in0=live["zb", i][:].rearrange("p (u m) -> p u m", u=4),
                 scalar1=rn[:, i : i + 1],
@@ -181,16 +189,8 @@ def tile_modelgraphpolicy_pb_t_kernel(tc, xum, action, up_w3, up_b3, dyn_w1_mu, 
             )
 
         def normalise(k):
-            scale(2 * k)
-            if k < NP - 1:
-                scale(2 * k + 1)
-            else:
-                nc.scalar.activation(
-                    out=mu_all[:, 2 * k + 1, :, 0:MSG],
-                    in_=live["zb", 2 * k + 1][:].rearrange("p (u m) -> p u m", u=4),
-                    func=ACT.Copy,
-                    scale=rn[:, 2 * k + 1 : 2 * k + 2],
-                )
+            for i in (2 * k, 2 * k + 1):
+                scale(i, nc.gpsimd if k < NP - 1 else nc.vector)
 
         def tr_m(i):
             bank = ps_t.tile([P, 4, P], F32, name="tm%d" % i, tag="t")
@@ -240,7 +240,7 @@ def tile_modelgraphpolicy_pb_t_kernel(tc, xum, action, up_w3, up_b3, dyn_w1_mu, 
             if a == 0:
                 live["ot", k] = four.tile([P, 2, F1], F32, name="ot%d" % k, tag="ot")
             nc.vector.tensor_tensor(
-                out=live["ot", k][:, a, :], in0=live["acc", i][:], in1=bias[:, 1024:1536], op=ALU.add
+                out=live["ot", k][:, a, :], in0=live["acc", i][:], in1=bias1[:], op=ALU.add
             )
 
         def relu_s(k, a):
@@ -254,17 +254,16 @@ def tile_modelgraphpolicy_pb_t_kernel(tc, xum, action, up_w3, up_b3, dyn_w1_mu, 
         def store(k, lo, hi):
             nc.sync.dma_start(out=o_v[:, 2 * k + lo : 2 * k + hi, :], in_=live["ot", k][:, lo:hi, :])
 
-        nc.vector.memset(brow[:].bitcast(I32), 0)
-        nc.vector.memset(ones[:], 1.0)
+        nc.vector.memset(brow3[:].bitcast(I32), 0)
         nc.vector.memset(warm[:], 1.0)
+        nc.vector.memset(ones[:], 1.0)
         nc.scalar.activation(out=warm[:], in_=warm[:], func=ACT.Abs_reciprocal_sqrt)
         make_identity(nc, ident[:])
 
         nc.sync.dma_start(out=x_all[:, 0:2, :], in_=x_v[:, 0:2, :])
-        nc.sync.dma_start(out=w3_raw[:, 0:4, :], in_=w3_v[:, 0:4, :])
-        nc.sync.dma_start(out=w3_raw[:, 4:7, :], in_=w3_v[:, 4:7, :])
-        nc.sync.dma_start(out=brow[0:1, 0:M], in_=up_b3.unsqueeze(0))
-        nc.sync.dma_start(out=brow[0:1, 1024:1536], in_=dyn_b1.unsqueeze(0))
+        nc.sync.dma_start(out=brow3[0:1, :], in_=up_b3.unsqueeze(0))
+        for lo, hi in ((0, 2), (2, 4), (4, 7)):
+            nc.sync.dma_start(out=w3_raw[:, lo:hi, :], in_=w3_v[:, lo:hi, :])
         nc.sync.dma_start(out=x_all[:, 2:4, :], in_=x_v[:, 2:4, :])
         nc.sync.dma_start(out=act_all[:, 0:4, :], in_=a_v[:, 0:4, :])
         nc.sync.dma_start(out=x_all[:, 4:8, :], in_=x_v[:, 4:8, :])
@@ -274,6 +273,7 @@ def tile_modelgraphpolicy_pb_t_kernel(tc, xum, action, up_w3, up_b3, dyn_w1_mu, 
                 in_=dyn_w1_mu[P * r : P * r + P, 0:M].rearrange("p (u m) -> p u m", u=4),
             )
         nc.sync.dma_start(out=w1a[:], in_=dyn_w1_mu[:, M : M + A].rearrange("(r p) a -> p r a", p=P))
+        nc.sync.dma_start(out=bias1[:], in_=dyn_b1.partition_broadcast(P))
         nc.sync.dma_start(out=act_all[:, 4:NT, :], in_=a_v[:, 4:NT, :])
         nc.sync.dma_start(out=x_all[:, 8:16, :], in_=x_v[:, 8:16, :])
         nc.sync.dma_start(out=x_all[:, 16:24, :], in_=x_v[:, 16:24, :])
@@ -281,66 +281,68 @@ def tile_modelgraphpolicy_pb_t_kernel(tc, xum, action, up_w3, up_b3, dyn_w1_mu, 
 
         tr_x(0)
         ex_x(0)
+        for lo, hi in ((0, 512), (512, M)):
+            spread(brow3[:, lo:hi], bias3[:, lo:hi], nc.vector.tensor_copy)
         tr_w3(0, ps_t, "t")
+        ex_w3(0, nc.vector.tensor_copy)
         tr_w3(1, ps_t, "t")
+        ex_w3(1, nc.scalar.copy)
+        q_x(0)
         tr_w3(2, ps_z, "z")
         tr_w3(3, ps_z, "z")
         tr_x(1)
-        ex_w3(0, nc.vector.tensor_copy)
-        ex_w3(1, nc.scalar.copy)
-        q_x(0)
         quantise(w3g[:, 0:4, :, :].rearrange("p a n t -> p (a n t)"), w3c[:, 0:512], w3s[:, 0:512])
-        ex_w3(2, nc.vector.tensor_copy)
-        ex_w3(3, nc.scalar.copy)
+        ex_w3(2, nc.scalar.copy)
         quantise(w3g[:, 4:6, :, :].rearrange("p a n t -> p (a n t)"), w3c[:, 512:768], w3s[:, 512:768])
+        ex_w3(3, nc.scalar.copy)
         quantise(w3g[:, 6:7, :, :].rearrange("p a n t -> p (a n t)"), w3c[:, 768:896], w3s[:, 768:896])
         ex_x(1)
-        for b, (pool, tag, copy) in enumerate(
-            ((ps_z, "z", nc.vector.tensor_copy), (ps_o, "o", nc.scalar.copy), (ps_o, "o", nc.scalar.copy))
-        ):
-            spread = pool.tile([P, 512], F32, name="spread%d" % b, tag=tag)
-            nc.tensor.matmul(out=spread[:], lhsT=ones[:], rhs=brow[:, 512 * b : 512 * b + 512], start=True, stop=True)
-            copy(out=bias[:, 512 * b : 512 * b + 512], in_=spread[:])
         z_lo(0)
         z_hi(0)
         z_lo(1)
-        q_x(1)
-        tr_x(2)
-        shuffle_action(mu_all, act_all, 0, 4)
-        shuffle_action(w1p, w1a, 0, NW1)
+        z_hi(1)
+        shuffle_action(nc.gpsimd, mu_all, act_all, 0, 4)
+        shuffle_action(nc.gpsimd, w1p, w1a, 0, NW1)
 
         def there(k):
             return 0 <= k < NP
 
         for k in range(NP + 3):
-            if there(k - 1):
-                norm_factor(k - 1)
             if there(k):
                 add_b3(2 * k)
+            if there(k - 1):
+                norm_factor(k - 1)
             if there(k - 3):
                 stage2(2 * k - 6)
                 stage2(2 * k - 5)
             if there(k):
-                z_hi(2 * k + 1)
                 add_b3(2 * k + 1)
+            if there(k + 2):
+                tr_x(k + 2)
+            if k == 0:
+                q_x(1)
             if 1 <= k <= 2:
                 ex_w1(2 * k - 2, nc.vector.tensor_copy)
+            if k == 1:
+                shuffle_action(nc.vector, mu_all, act_all, 4, NT)
+            if k == 2:
+                ex_w1(3, nc.vector.tensor_copy)
+            if k == NP:
+                normalise(k - 1)
             if k == NP + 1:
                 ex_m(k - 2)
                 q_m(k - 2)
             if there(k - 3):
                 add_b1(2 * k - 6)
                 add_b1(2 * k - 5)
-            if there(k - 1) and k == NP:
-                normalise(k - 1)
             if there(k - 2) and k <= NP:
                 ex_m(k - 2)
             if there(k):
                 squares(2 * k)
             if there(k + 2):
                 ex_x(k + 2)
-            if 1 <= k <= 2:
-                ex_w1(2 * k - 1, nc.scalar.copy)
+            if k == 1:
+                ex_w1(1, nc.scalar.copy)
             if there(k):
                 squares(2 * k + 1)
             if there(k - 1) and k < NP:
@@ -349,14 +351,16 @@ def tile_modelgraphpolicy_pb_t_kernel(tc, xum, action, up_w3, up_b3, dyn_w1_mu, 
                 z_lo(2 * k + 2)
                 z_hi(2 * k + 2)
                 z_lo(2 * k + 3)
+                z_hi(2 * k + 3)
+            if k == 1:
+                tr_w1(2)
+                tr_w1(3)
             if there(k - 1):
                 tr_m(2 * k - 2)
                 tr_m(2 * k - 1)
-            if there(k + 3):
-                tr_x(k + 3)
-            if k < 2:
-                tr_w1(2 * k)
-                tr_w1(2 * k + 1)
+            if k == 0:
+                tr_w1(0)
+                tr_w1(1)
             if there(k - 2) and k <= NP:
                 q_m(k - 2)
             if there(k + 2):
@@ -367,7 +371,10 @@ def tile_modelgraphpolicy_pb_t_kernel(tc, xum, action, up_w3, up_b3, dyn_w1_mu, 
             if there(k):
                 root(k)
             if there(k - 4) and k - 4 < NP - 1:
-                relu_v(k - 4, 0)
+                if k < NP:
+                    relu_v(k - 4, 0)
+                else:
+                    relu_s(k - 4, 0)
                 relu_s(k - 4, 1)
                 store(k - 4, 0, 2)
             if k - 3 == NP - 1:
@@ -375,5 +382,3 @@ def tile_modelgraphpolicy_pb_t_kernel(tc, xum, action, up_w3, up_b3, dyn_w1_mu, 
                 store(k - 3, 0, 1)
                 relu_v(k - 3, 1)
                 store(k - 3, 1, 2)
-            if k < 4:
-                shuffle_action(mu_all, act_all, 4 + 7 * k, 11 + 7 * k)

@@ -273,9 +273,9 @@ def tile_modelgraphpolicy_pb_t_kernel(tc, xum, action, up_w3, up_b3, dyn_w1_mu, 
                 in_=dyn_w1_mu[P * r : P * r + P, 0:M].rearrange("p (u m) -> p u m", u=4),
             )
         nc.sync.dma_start(out=w1a[:], in_=dyn_w1_mu[:, M : M + A].rearrange("(r p) a -> p r a", p=P))
-        nc.sync.dma_start(out=bias1[:], in_=dyn_b1.partition_broadcast(P))
-        nc.sync.dma_start(out=act_all[:, 4:NT, :], in_=a_v[:, 4:NT, :])
         nc.sync.dma_start(out=x_all[:, 8:16, :], in_=x_v[:, 8:16, :])
+        nc.sync.dma_start(out=act_all[:, 4:NT, :], in_=a_v[:, 4:NT, :])
+        nc.sync.dma_start(out=bias1[:], in_=dyn_b1.partition_broadcast(P))
         nc.sync.dma_start(out=x_all[:, 16:24, :], in_=x_v[:, 16:24, :])
         nc.sync.dma_start(out=x_all[:, 24:32, :], in_=x_v[:, 24:32, :])
 
@@ -308,23 +308,23 @@ def tile_modelgraphpolicy_pb_t_kernel(tc, xum, action, up_w3, up_b3, dyn_w1_mu, 
             return 0 <= k < NP
 
         for k in range(NP + 3):
+            if there(k + 2):
+                tr_x(k + 2)
+            if k >= 3 and there(k - 1):
+                norm_factor(k - 1)
             if there(k):
                 add_b3(2 * k)
-            if there(k - 1):
+            if 1 <= k < 3:
                 norm_factor(k - 1)
             if there(k - 3):
                 stage2(2 * k - 6)
                 stage2(2 * k - 5)
             if there(k):
                 add_b3(2 * k + 1)
-            if there(k + 2):
-                tr_x(k + 2)
             if k == 0:
                 q_x(1)
             if 1 <= k <= 2:
                 ex_w1(2 * k - 2, nc.vector.tensor_copy)
-            if k == 1:
-                shuffle_action(nc.vector, mu_all, act_all, 4, NT)
             if k == 2:
                 ex_w1(3, nc.vector.tensor_copy)
             if k == NP:
@@ -366,6 +366,7 @@ def tile_modelgraphpolicy_pb_t_kernel(tc, xum, action, up_w3, up_b3, dyn_w1_mu, 
             if there(k + 2):
                 q_x(k + 2)
             if k == 2:
+                shuffle_action(nc.vector, mu_all, act_all, 4, NT)
                 for c in range(2):
                     quantise(w1g[:, c, :, :].rearrange("p f t -> p (f t)"), w1c[:, c, :], w1s[:, c, :])
             if there(k):

@@ -18,8 +18,7 @@ NT = B // P
 NP = NT // 2
 NW3 = M // P
 NW1 = F1 // P
-MSG = 224
-ACO = 32
+K2 = M + A
 RMAX = 1e12
 
 FLOPS = 2 * B * H * M + 2 * B * (M + A) * F1
@@ -32,8 +31,8 @@ def tile_modelgraphpolicy_pb_t_kernel(tc, xum, action, up_w3, up_b3, dyn_w1_mu, 
         two = ctx.enter_context(tc.tile_pool(name="two", bufs=2))
         four = ctx.enter_context(tc.tile_pool(name="four", bufs=4))
         six = ctx.enter_context(tc.tile_pool(name="six", bufs=6))
-        ps_z = ctx.enter_context(tc.psum_pool(name="ps_z", bufs=4))
-        ps_t = ctx.enter_context(tc.psum_pool(name="ps_t", bufs=2))
+        ps_z = ctx.enter_context(tc.psum_pool(name="ps_z", bufs=3))
+        ps_t = ctx.enter_context(tc.psum_pool(name="ps_t", bufs=3))
         ps_o = ctx.enter_context(tc.psum_pool(name="ps_o", bufs=2))
         ctx.enter_context(tc.manual_schedule())
 
@@ -44,17 +43,15 @@ def tile_modelgraphpolicy_pb_t_kernel(tc, xum, action, up_w3, up_b3, dyn_w1_mu, 
         bias1 = keep.tile([P, F1], BF16, name="bias1")
         warm = keep.tile([P, 1], F32, name="warm")
         x_all = keep.tile([P, NT, H], BF16, name="x_all")
-        act_all = keep.tile([P, NT, A], BF16, name="act_all")
         w3_raw = keep.tile([P, NW3, H], BF16, name="w3_raw")
-        w1p = keep.tile([P, NW1, 4, MSG + ACO], BF16, name="w1p")
-        w1a = keep.tile([P, NW1, A], BF16, name="w1a")
+        w1_raw = keep.tile([P, NW1, K2], BF16, name="w1_raw")
         w3g = keep.tile([P, NW3, P, 4], BF16, name="w3g", align_bytes=64)
         w1g = keep.tile([P, 2, F1, 4], BF16, name="w1g", align_bytes=64)
         w3c = keep.tile([P, M], U32, name="w3c", align_bytes=64)
         w3s = keep.tile([P, M], U8, name="w3s", align_bytes=64)
         w1c = keep.tile([P, 2, F1], U32, name="w1c", align_bytes=64)
         w1s = keep.tile([P, 2, F1], U8, name="w1s", align_bytes=64)
-        mu_all = keep.tile([P, NT, 4, MSG + ACO], BF16, name="mu_all")
+        mu_all = keep.tile([P, NT, K2], BF16, name="mu_all")
         xc = keep.tile([P, NT, P], U32, name="xc", align_bytes=64)
         xs = keep.tile([P, NT, P], U8, name="xs", align_bytes=64)
         ss = keep.tile([P, NT], F32, name="ss")
@@ -81,18 +78,9 @@ def tile_modelgraphpolicy_pb_t_kernel(tc, xum, action, up_w3, up_b3, dyn_w1_mu, 
         def quantise(grouped, codes, scales):
             nc.vector.quantize_mx(out=codes.bitcast(FP8X4), scales=scales, in_=grouped)
 
-        def shuffle_action(engine, dst4, src, lo, hi):
-            dst = dst4[:].rearrange("p i (c h) m -> p (i c) h m", h=2)
-            srv = src[:].rearrange("p i (c g h j) -> p (i c) g h j", c=2, g=2, h=2)
-            for h in range(2):
-                engine.tensor_scalar(
-                    out=dst[:, 2 * lo : 2 * hi, h, MSG : MSG + ACO].rearrange("p a (g j) -> p a g j", g=2),
-                    in0=srv[:, 2 * lo : 2 * hi, :, h, :],
-                    scalar1=1.0,
-                    scalar2=0.0,
-                    op0=ALU.mult,
-                    op1=ALU.add,
-                )
+        def row_words(row):
+            words = row.bitcast(F32)
+            return [words[:, 0:128], words[:, 128:256], words[:, 256:512:2], words[:, 257:512:2]]
 
         def tr_x(k):
             bank = ps_t.tile([P, 4, P], F32, name="tx%d" % k, tag="t")
@@ -135,7 +123,7 @@ def tile_modelgraphpolicy_pb_t_kernel(tc, xum, action, up_w3, up_b3, dyn_w1_mu, 
 
         def tr_w1(r):
             bank = ps_o.tile([P, 4, P], F32, name="tw1%d" % r, tag="o")
-            transpose_words(bank, [w1p[:, r, u, :].bitcast(F32) for u in range(4)])
+            transpose_words(bank, row_words(w1_raw[:, r, :]))
             live["tw1", r] = bank
 
         def ex_w1(r, copy):
@@ -161,10 +149,21 @@ def tile_modelgraphpolicy_pb_t_kernel(tc, xum, action, up_w3, up_b3, dyn_w1_mu, 
             z_pass(i, zc[:, 0:256], 512, 768)
             z_pass(i, zc[:, 256:384], 768, 896)
 
-        def add_b3(i):
+        def add_lo(i):
             live["zb", i] = zb = six.tile([P, M], F32, name="zb%d" % i, tag="zb")
             nc.vector.tensor_tensor(out=zb[:, 0:512], in0=live["za", i][:], in1=bias3[:, 0:512], op=ALU.add)
+
+        def add_hi(i):
+            zb = live["zb", i]
             nc.vector.tensor_tensor(out=zb[:, 512:896], in0=live["zc", i][:, 0:384], in1=bias3[:, 512:896], op=ALU.add)
+
+        def add_b3(i):
+            add_lo(i)
+            add_hi(i)
+
+        def z_a(k):
+            z_lo(2 * k)
+            z_hi(2 * k)
 
         def squares(i):
             junk = two.tile([P, M], BF16, name="junk%d" % i, tag="junk")
@@ -180,8 +179,8 @@ def tile_modelgraphpolicy_pb_t_kernel(tc, xum, action, up_w3, up_b3, dyn_w1_mu, 
 
         def scale(i, engine):
             engine.tensor_scalar(
-                out=mu_all[:, i, :, 0:MSG],
-                in0=live["zb", i][:].rearrange("p (u m) -> p u m", u=4),
+                out=mu_all[:, i, 0:M],
+                in0=live["zb", i][:],
                 scalar1=rn[:, i : i + 1],
                 scalar2=0.0,
                 op0=ALU.mult,
@@ -194,7 +193,7 @@ def tile_modelgraphpolicy_pb_t_kernel(tc, xum, action, up_w3, up_b3, dyn_w1_mu, 
 
         def tr_m(i):
             bank = ps_t.tile([P, 4, P], F32, name="tm%d" % i, tag="t")
-            transpose_words(bank, [mu_all[:, i, u, :].bitcast(F32) for u in range(4)])
+            transpose_words(bank, row_words(mu_all[:, i, :]))
             live["tm", i] = bank
 
         def ex_m(k):
@@ -243,9 +242,9 @@ def tile_modelgraphpolicy_pb_t_kernel(tc, xum, action, up_w3, up_b3, dyn_w1_mu, 
                 out=live["ot", k][:, a, :], in0=live["acc", i][:], in1=bias1[:], op=ALU.add
             )
 
-        def relu_s(k, a):
+        def relu_s(k, a, lo, hi):
             ot = live["ot", k]
-            nc.scalar.activation(out=ot[:, a, :], in_=ot[:, a, :], func=ACT.Relu)
+            nc.scalar.activation(out=ot[:, a, lo:hi], in_=ot[:, a, lo:hi], func=ACT.Relu)
 
         def relu_v(k, a):
             ot = live["ot", k]
@@ -265,17 +264,12 @@ def tile_modelgraphpolicy_pb_t_kernel(tc, xum, action, up_w3, up_b3, dyn_w1_mu, 
         for lo, hi in ((0, 2), (2, 4), (4, 7)):
             nc.sync.dma_start(out=w3_raw[:, lo:hi, :], in_=w3_v[:, lo:hi, :])
         nc.sync.dma_start(out=x_all[:, 2:4, :], in_=x_v[:, 2:4, :])
-        nc.sync.dma_start(out=act_all[:, 0:4, :], in_=a_v[:, 0:4, :])
         nc.sync.dma_start(out=x_all[:, 4:8, :], in_=x_v[:, 4:8, :])
-        for r in range(NW1):
-            nc.sync.dma_start(
-                out=w1p[:, r, :, 0:MSG],
-                in_=dyn_w1_mu[P * r : P * r + P, 0:M].rearrange("p (u m) -> p u m", u=4),
-            )
-        nc.sync.dma_start(out=w1a[:], in_=dyn_w1_mu[:, M : M + A].rearrange("(r p) a -> p r a", p=P))
+        nc.sync.dma_start(out=w1_raw[:], in_=dyn_w1_mu.rearrange("(r p) k -> p r k", p=P))
+        nc.sync.dma_start(out=mu_all[:, 0:8, M:K2], in_=a_v[:, 0:8, :])
         nc.sync.dma_start(out=x_all[:, 8:16, :], in_=x_v[:, 8:16, :])
-        nc.sync.dma_start(out=act_all[:, 4:NT, :], in_=a_v[:, 4:NT, :])
         nc.sync.dma_start(out=bias1[:], in_=dyn_b1.partition_broadcast(P))
+        nc.sync.dma_start(out=mu_all[:, 8:NT, M:K2], in_=a_v[:, 8:NT, :])
         nc.sync.dma_start(out=x_all[:, 16:24, :], in_=x_v[:, 16:24, :])
         nc.sync.dma_start(out=x_all[:, 24:32, :], in_=x_v[:, 24:32, :])
 
@@ -297,89 +291,132 @@ def tile_modelgraphpolicy_pb_t_kernel(tc, xum, action, up_w3, up_b3, dyn_w1_mu, 
         ex_w3(3, nc.scalar.copy)
         quantise(w3g[:, 6:7, :, :].rearrange("p a n t -> p (a n t)"), w3c[:, 768:896], w3s[:, 768:896])
         ex_x(1)
-        z_lo(0)
-        z_hi(0)
+        q_x(1)
+        z_a(0)
         z_lo(1)
+        tr_x(2)
+
+        add_b3(0)
         z_hi(1)
-        shuffle_action(nc.gpsimd, mu_all, act_all, 0, 4)
-        shuffle_action(nc.gpsimd, w1p, w1a, 0, NW1)
+        ex_x(2)
+        squares(0)
+        add_b3(1)
+        squares(1)
+        root(0)
+        z_a(1)
+        z_lo(3)
+        q_x(2)
+        tr_x(3)
+        tr_w1(0)
+        tr_w1(1)
 
-        def there(k):
-            return 0 <= k < NP
+        add_b3(2)
+        z_hi(3)
+        ex_x(3)
+        squares(2)
+        add_b3(3)
+        q_x(3)
+        norm_factor(0)
+        normalise(0)
+        ex_w1(0, nc.vector.tensor_copy)
+        ex_w1(1, nc.scalar.copy)
+        squares(3)
+        root(1)
+        z_a(2)
+        z_lo(5)
+        tr_w1(2)
+        tr_w1(3)
+        tr_m(0)
+        add_lo(4)
+        z_hi(5)
+        tr_m(1)
+        tr_x(4)
 
-        for k in range(NP + 3):
-            if there(k + 2):
-                tr_x(k + 2)
-            if k >= 3 and there(k - 1):
-                norm_factor(k - 1)
-            if there(k):
-                add_b3(2 * k)
-            if 1 <= k < 3:
-                norm_factor(k - 1)
-            if there(k - 3):
-                stage2(2 * k - 6)
-                stage2(2 * k - 5)
-            if there(k):
-                add_b3(2 * k + 1)
-            if k == 0:
-                q_x(1)
-            if 1 <= k <= 2:
-                ex_w1(2 * k - 2, nc.vector.tensor_copy)
-            if k == 2:
-                ex_w1(3, nc.vector.tensor_copy)
-            if k == NP:
-                normalise(k - 1)
-            if k == NP + 1:
-                ex_m(k - 2)
-                q_m(k - 2)
-            if there(k - 3):
-                add_b1(2 * k - 6)
-                add_b1(2 * k - 5)
-            if there(k - 2) and k <= NP:
-                ex_m(k - 2)
-            if there(k):
-                squares(2 * k)
-            if there(k + 2):
+        add_hi(4)
+        norm_factor(1)
+        add_b3(5)
+        normalise(1)
+        squares(4)
+        ex_m(0)
+        squares(5)
+        ex_x(4)
+        ex_w1(2, nc.vector.tensor_copy)
+        ex_w1(3, nc.vector.tensor_copy)
+        z_a(3)
+        z_lo(7)
+        tr_m(2)
+        tr_m(3)
+        tr_x(5)
+        q_m(0)
+        for c in range(2):
+            quantise(w1g[:, c, :, :].rearrange("p f t -> p (f t)"), w1c[:, c, :], w1s[:, c, :])
+        q_x(4)
+        root(2)
+
+        for k in range(3, NP):
+            a, b = 2 * k, 2 * k + 1
+            norm_factor(k - 1)
+            add_b3(a)
+            stage2(a - 6)
+            z_hi(b)
+            add_b3(b)
+            stage2(b - 6)
+            add_b1(a - 6)
+            add_b1(b - 6)
+            ex_m(k - 2)
+            if k + 2 < NP:
                 ex_x(k + 2)
-            if k == 1:
-                ex_w1(1, nc.scalar.copy)
-            if there(k):
-                squares(2 * k + 1)
-            if there(k - 1) and k < NP:
-                normalise(k - 1)
-            if there(k + 1):
-                z_lo(2 * k + 2)
-                z_hi(2 * k + 2)
-                z_lo(2 * k + 3)
-                z_hi(2 * k + 3)
-            if k == 1:
-                tr_w1(2)
-                tr_w1(3)
-            if there(k - 1):
-                tr_m(2 * k - 2)
-                tr_m(2 * k - 1)
-            if k == 0:
-                tr_w1(0)
-                tr_w1(1)
-            if there(k - 2) and k <= NP:
-                q_m(k - 2)
-            if there(k + 2):
+            squares(a)
+            squares(b)
+            normalise(k - 1)
+            if k + 1 < NP:
+                z_a(k + 1)
+                z_lo(b + 2)
+            tr_m(a - 2)
+            tr_m(b - 2)
+            if k + 3 < NP:
+                tr_x(k + 3)
+            q_m(k - 2)
+            if k + 2 < NP:
                 q_x(k + 2)
-            if k == 2:
-                shuffle_action(nc.vector, mu_all, act_all, 4, NT)
-                for c in range(2):
-                    quantise(w1g[:, c, :, :].rearrange("p f t -> p (f t)"), w1c[:, c, :], w1s[:, c, :])
-            if there(k):
-                root(k)
-            if there(k - 4) and k - 4 < NP - 1:
-                if k < NP:
-                    relu_v(k - 4, 0)
-                else:
-                    relu_s(k - 4, 0)
-                relu_s(k - 4, 1)
+            if k > 3:
+                relu_v(k - 4, 0)
+                relu_s(k - 4, 1, 0, F1 // 2)
+            root(k)
+            if k > 3:
+                relu_s(k - 4, 1, F1 // 2, F1)
                 store(k - 4, 0, 2)
-            if k - 3 == NP - 1:
-                relu_s(k - 3, 0)
-                store(k - 3, 0, 1)
-                relu_v(k - 3, 1)
-                store(k - 3, 1, 2)
+
+        ex_m(NP - 2)
+        norm_factor(NP - 1)
+        normalise(NP - 1)
+        stage2(NT - 6)
+        stage2(NT - 5)
+        tr_m(NT - 2)
+        tr_m(NT - 1)
+        q_m(NP - 2)
+        add_b1(NT - 6)
+        add_b1(NT - 5)
+        relu_s(NP - 4, 0, 0, F1)
+        relu_s(NP - 4, 1, 0, F1)
+        store(NP - 4, 0, 2)
+        ex_m(NP - 1)
+        q_m(NP - 1)
+        stage2(NT - 4)
+        stage2(NT - 3)
+        add_b1(NT - 4)
+        add_b1(NT - 3)
+        relu_s(NP - 3, 0, 0, F1)
+        relu_s(NP - 3, 1, 0, F1)
+        store(NP - 3, 0, 2)
+        stage2(NT - 2)
+        stage2(NT - 1)
+        add_b1(NT - 2)
+        add_b1(NT - 1)
+        relu_s(NP - 2, 0, 0, F1)
+        relu_s(NP - 2, 1, 0, F1)
+        store(NP - 2, 0, 2)
+        relu_s(NP - 1, 0, 0, F1)
+        store(NP - 1, 0, 1)
+        relu_v(NP - 1, 1)
+        store(NP - 1, 1, 2)

@@ -196,10 +196,14 @@ def tile_modelgraphpolicy_pb_t_kernel(tc, xum, action, up_w3, up_b3, dyn_w1_mu, 
             transpose_words(bank, row_words(mu_all[:, i, :]))
             live["tm", i] = bank
 
+        def ex_m1(k, a):
+            if a == 0:
+                live["mug", k] = two.tile([P, 2, 2, P, 4], BF16, name="mug%d" % k, tag="mug", align_bytes=64)
+            leave_bank(nc.scalar.copy, live["mug", k][:, a, :, :, :], live["tm", 2 * k + a], 2)
+
         def ex_m(k):
-            live["mug", k] = mug = two.tile([P, 2, 2, P, 4], BF16, name="mug%d" % k, tag="mug", align_bytes=64)
-            for a in range(2):
-                leave_bank(nc.scalar.copy, mug[:, a, :, :, :], live["tm", 2 * k + a], 2)
+            ex_m1(k, 0)
+            ex_m1(k, 1)
 
         def q_m(k):
             live["muc", k] = muc = two.tile([P, 2, 2, P], U32, name="muc%d" % k, tag="muc", align_bytes=64)
@@ -275,70 +279,73 @@ def tile_modelgraphpolicy_pb_t_kernel(tc, xum, action, up_w3, up_b3, dyn_w1_mu, 
 
         tr_x(0)
         ex_x(0)
-        for lo, hi in ((0, 512), (512, M)):
-            spread(brow3[:, lo:hi], bias3[:, lo:hi], nc.vector.tensor_copy)
         tr_w3(0, ps_t, "t")
         ex_w3(0, nc.vector.tensor_copy)
         tr_w3(1, ps_t, "t")
         ex_w3(1, nc.scalar.copy)
         q_x(0)
         tr_w3(2, ps_z, "z")
-        tr_w3(3, ps_z, "z")
-        tr_x(1)
-        quantise(w3g[:, 0:4, :, :].rearrange("p a n t -> p (a n t)"), w3c[:, 0:512], w3s[:, 0:512])
         ex_w3(2, nc.scalar.copy)
+        quantise(w3g[:, 0:4, :, :].rearrange("p a n t -> p (a n t)"), w3c[:, 0:512], w3s[:, 0:512])
+        tr_w3(3, ps_z, "z")
+        ex_w3(3, nc.vector.tensor_copy)
+        tr_x(1)
+        spread(brow3[:, 0:512], bias3[:, 0:512], nc.scalar.copy)
+        spread(brow3[:, 512:M], bias3[:, 512:M], nc.vector.tensor_copy)
         quantise(w3g[:, 4:6, :, :].rearrange("p a n t -> p (a n t)"), w3c[:, 512:768], w3s[:, 512:768])
-        ex_w3(3, nc.scalar.copy)
         quantise(w3g[:, 6:7, :, :].rearrange("p a n t -> p (a n t)"), w3c[:, 768:896], w3s[:, 768:896])
         ex_x(1)
-        q_x(1)
         z_a(0)
         z_lo(1)
         tr_x(2)
 
-        add_b3(0)
+        add_lo(0)
+        q_x(1)
+        add_hi(0)
         z_hi(1)
-        ex_x(2)
         squares(0)
+        ex_x(2)
         add_b3(1)
         squares(1)
-        root(0)
         z_a(1)
         z_lo(3)
-        q_x(2)
         tr_x(3)
-        tr_w1(0)
-        tr_w1(1)
 
         add_b3(2)
         z_hi(3)
-        ex_x(3)
-        squares(2)
+        tr_w1(0)
+        tr_w1(1)
         add_b3(3)
-        q_x(3)
-        norm_factor(0)
-        normalise(0)
+        q_x(2)
+        ex_x(3)
+        root(0)
         ex_w1(0, nc.vector.tensor_copy)
-        ex_w1(1, nc.scalar.copy)
+        squares(2)
         squares(3)
         root(1)
+        norm_factor(0)
+        q_x(3)
+        normalise(0)
         z_a(2)
         z_lo(5)
+        ex_w1(1, nc.vector.tensor_copy)
+        add_lo(4)
+        z_hi(5)
         tr_w1(2)
         tr_w1(3)
         tr_m(0)
-        add_lo(4)
-        z_hi(5)
         tr_m(1)
         tr_x(4)
-
         add_hi(4)
+
+        squares(4)
         norm_factor(1)
         add_b3(5)
         normalise(1)
-        squares(4)
-        ex_m(0)
+        ex_m1(0, 0)
         squares(5)
+        ex_m1(0, 1)
+        root(2)
         ex_x(4)
         ex_w1(2, nc.vector.tensor_copy)
         ex_w1(3, nc.vector.tensor_copy)
@@ -347,11 +354,10 @@ def tile_modelgraphpolicy_pb_t_kernel(tc, xum, action, up_w3, up_b3, dyn_w1_mu, 
         tr_m(2)
         tr_m(3)
         tr_x(5)
-        q_m(0)
         for c in range(2):
             quantise(w1g[:, c, :, :].rearrange("p f t -> p (f t)"), w1c[:, c, :], w1s[:, c, :])
+        q_m(0)
         q_x(4)
-        root(2)
 
         for k in range(3, NP):
             a, b = 2 * k, 2 * k + 1
@@ -407,15 +413,17 @@ def tile_modelgraphpolicy_pb_t_kernel(tc, xum, action, up_w3, up_b3, dyn_w1_mu, 
         add_b1(NT - 4)
         add_b1(NT - 3)
         relu_s(NP - 3, 0, 0, F1)
+        store(NP - 3, 0, 1)
         relu_s(NP - 3, 1, 0, F1)
-        store(NP - 3, 0, 2)
+        store(NP - 3, 1, 2)
         stage2(NT - 2)
         stage2(NT - 1)
         add_b1(NT - 2)
         add_b1(NT - 1)
         relu_s(NP - 2, 0, 0, F1)
+        store(NP - 2, 0, 1)
         relu_s(NP - 2, 1, 0, F1)
-        store(NP - 2, 0, 2)
+        store(NP - 2, 1, 2)
         relu_s(NP - 1, 0, 0, F1)
         store(NP - 1, 0, 1)
         relu_v(NP - 1, 1)

@@ -37,7 +37,7 @@ def tile_modelgraphpolicy_pb_t_kernel(tc, xum, action, up_w3, up_b3, dyn_w1_mu, 
         ctx.enter_context(tc.manual_schedule())
 
         ident = keep.tile([P, P], F32, name="ident")
-        ones = keep.tile([P, P], BF16, name="ones")
+        ones = keep.tile([P, 512], BF16, name="ones")
         brow3 = keep.tile([P, M], BF16, name="brow3")
         bias3 = keep.tile([P, M], F32, name="bias3")
         bias1 = keep.tile([P, F1], BF16, name="bias1")
@@ -118,8 +118,13 @@ def tile_modelgraphpolicy_pb_t_kernel(tc, xum, action, up_w3, up_b3, dyn_w1_mu, 
         def spread(row, wide, copy):
             bank = ps_o.tile([P, 512], F32, name="spread", tag="o")
             n = row.shape[1]
-            nc.tensor.matmul(out=bank[:, 0:n], lhsT=ones[:], rhs=row, start=True, stop=True)
+            nc.tensor.matmul(out=bank[:, 0:n], lhsT=ones[:, 0:P], rhs=row, start=True, stop=True)
             copy(out=wide, in_=bank[:, 0:n])
+
+        def keep_clock(n):
+            bank = ps_o.tile([P, 512], F32, name="clock", tag="o")
+            for r in range(n):
+                nc.tensor.matmul(out=bank[:], lhsT=ones[:, 0:P], rhs=ones[:], start=True, stop=True)
 
         def tr_w1(r):
             bank = ps_o.tile([P, 4, P], F32, name="tw1%d" % r, tag="o")
@@ -246,13 +251,16 @@ def tile_modelgraphpolicy_pb_t_kernel(tc, xum, action, up_w3, up_b3, dyn_w1_mu, 
                 out=live["ot", k][:, a, :], in0=live["acc", i][:], in1=bias1[:], op=ALU.add
             )
 
-        def relu_s(k, a, lo, hi):
-            ot = live["ot", k]
-            nc.scalar.activation(out=ot[:, a, lo:hi], in_=ot[:, a, lo:hi], func=ACT.Relu)
+        def pair_columns(k, lo, hi):
+            return live["ot", k][:].rearrange("p a f -> p (a f)")[:, lo:hi]
 
-        def relu_v(k, a):
-            ot = live["ot", k]
-            nc.vector.tensor_scalar_max(out=ot[:, a, :], in0=ot[:, a, :], scalar1=0.0)
+        def relu_s(k, lo, hi):
+            cols = pair_columns(k, lo, hi)
+            nc.scalar.activation(out=cols, in_=cols, func=ACT.Relu)
+
+        def relu_v(k, lo, hi):
+            cols = pair_columns(k, lo, hi)
+            nc.vector.tensor_scalar_max(out=cols, in0=cols, scalar1=0.0)
 
         def store(k, lo, hi):
             nc.sync.dma_start(out=o_v[:, 2 * k + lo : 2 * k + hi, :], in_=live["ot", k][:, lo:hi, :])
@@ -277,6 +285,7 @@ def tile_modelgraphpolicy_pb_t_kernel(tc, xum, action, up_w3, up_b3, dyn_w1_mu, 
         nc.sync.dma_start(out=x_all[:, 16:24, :], in_=x_v[:, 16:24, :])
         nc.sync.dma_start(out=x_all[:, 24:32, :], in_=x_v[:, 24:32, :])
 
+        keep_clock(5)
         tr_x(0)
         ex_x(0)
         tr_w3(0, ps_t, "t")
@@ -284,18 +293,20 @@ def tile_modelgraphpolicy_pb_t_kernel(tc, xum, action, up_w3, up_b3, dyn_w1_mu, 
         tr_w3(1, ps_t, "t")
         ex_w3(1, nc.scalar.copy)
         q_x(0)
+        quantise(w3g[:, 0:2, :, :].rearrange("p a n t -> p (a n t)"), w3c[:, 0:256], w3s[:, 0:256])
+        spread(brow3[:, 0:512], bias3[:, 0:512], nc.vector.tensor_copy)
+        spread(brow3[:, 512:M], bias3[:, 512:M], nc.scalar.copy)
+        quantise(w3g[:, 2:4, :, :].rearrange("p a n t -> p (a n t)"), w3c[:, 256:512], w3s[:, 256:512])
         tr_w3(2, ps_z, "z")
         ex_w3(2, nc.scalar.copy)
-        quantise(w3g[:, 0:4, :, :].rearrange("p a n t -> p (a n t)"), w3c[:, 0:512], w3s[:, 0:512])
         tr_w3(3, ps_z, "z")
         ex_w3(3, nc.vector.tensor_copy)
         tr_x(1)
-        spread(brow3[:, 0:512], bias3[:, 0:512], nc.scalar.copy)
-        spread(brow3[:, 512:M], bias3[:, 512:M], nc.vector.tensor_copy)
+        z_lo(0)
         quantise(w3g[:, 4:6, :, :].rearrange("p a n t -> p (a n t)"), w3c[:, 512:768], w3s[:, 512:768])
         quantise(w3g[:, 6:7, :, :].rearrange("p a n t -> p (a n t)"), w3c[:, 768:896], w3s[:, 768:896])
         ex_x(1)
-        z_a(0)
+        z_hi(0)
         z_lo(1)
         tr_x(2)
 
@@ -386,11 +397,11 @@ def tile_modelgraphpolicy_pb_t_kernel(tc, xum, action, up_w3, up_b3, dyn_w1_mu, 
             if k + 2 < NP:
                 q_x(k + 2)
             if k > 3:
-                relu_v(k - 4, 0)
-                relu_s(k - 4, 1, 0, F1 // 2)
+                relu_v(k - 4, 0, 448)
+                relu_s(k - 4, 448, 704)
             root(k)
             if k > 3:
-                relu_s(k - 4, 1, F1 // 2, F1)
+                relu_s(k - 4, 704, 2 * F1)
                 store(k - 4, 0, 2)
 
         ex_m(NP - 2)
@@ -403,8 +414,8 @@ def tile_modelgraphpolicy_pb_t_kernel(tc, xum, action, up_w3, up_b3, dyn_w1_mu, 
         q_m(NP - 2)
         add_b1(NT - 6)
         add_b1(NT - 5)
-        relu_s(NP - 4, 0, 0, F1)
-        relu_s(NP - 4, 1, 0, F1)
+        relu_s(NP - 4, 0, F1)
+        relu_s(NP - 4, F1, 2 * F1)
         store(NP - 4, 0, 2)
         ex_m(NP - 1)
         q_m(NP - 1)
@@ -412,19 +423,19 @@ def tile_modelgraphpolicy_pb_t_kernel(tc, xum, action, up_w3, up_b3, dyn_w1_mu, 
         stage2(NT - 3)
         add_b1(NT - 4)
         add_b1(NT - 3)
-        relu_s(NP - 3, 0, 0, F1)
+        relu_s(NP - 3, 0, F1)
         store(NP - 3, 0, 1)
-        relu_s(NP - 3, 1, 0, F1)
+        relu_s(NP - 3, F1, 2 * F1)
         store(NP - 3, 1, 2)
         stage2(NT - 2)
         stage2(NT - 1)
         add_b1(NT - 2)
         add_b1(NT - 1)
-        relu_s(NP - 2, 0, 0, F1)
+        relu_s(NP - 2, 0, F1)
         store(NP - 2, 0, 1)
-        relu_s(NP - 2, 1, 0, F1)
+        relu_s(NP - 2, F1, 2 * F1)
         store(NP - 2, 1, 2)
-        relu_s(NP - 1, 0, 0, F1)
+        relu_s(NP - 1, 0, F1)
         store(NP - 1, 0, 1)
-        relu_v(NP - 1, 1)
+        relu_v(NP - 1, F1, 2 * F1)
         store(NP - 1, 1, 2)

@@ -362,9 +362,11 @@ def tile_modelgraphpolicy_pb_t_kernel(tc, xum, action, up_w3, up_b3, dyn_w1_mu, 
         ex_w1(3, nc.vector.tensor_copy)
         z_a(3)
         z_lo(7)
+        add_lo(6)
         tr_m(2)
         tr_m(3)
         tr_x(5)
+        z_hi(7)
         for c in range(2):
             quantise(w1g[:, c, :, :].rearrange("p f t -> p (f t)"), w1c[:, c, :], w1s[:, c, :])
         q_m(0)
@@ -373,13 +375,15 @@ def tile_modelgraphpolicy_pb_t_kernel(tc, xum, action, up_w3, up_b3, dyn_w1_mu, 
         for k in range(3, NP):
             a, b = 2 * k, 2 * k + 1
             norm_factor(k - 1)
-            add_b3(a)
+            add_hi(a)
             stage2(a - 6)
-            z_hi(b)
-            add_b3(b)
             stage2(b - 6)
+            add_b3(b)
             add_b1(a - 6)
             add_b1(b - 6)
+            if k + 1 < NP:
+                z_lo(a + 2)
+                add_lo(a + 2)
             ex_m(k - 2)
             if k + 2 < NP:
                 ex_x(k + 2)
@@ -387,12 +391,14 @@ def tile_modelgraphpolicy_pb_t_kernel(tc, xum, action, up_w3, up_b3, dyn_w1_mu, 
             squares(b)
             normalise(k - 1)
             if k + 1 < NP:
-                z_a(k + 1)
+                z_hi(a + 2)
                 z_lo(b + 2)
             tr_m(a - 2)
             tr_m(b - 2)
             if k + 3 < NP:
                 tr_x(k + 3)
+            if k + 1 < NP:
+                z_hi(b + 2)
             q_m(k - 2)
             if k + 2 < NP:
                 q_x(k + 2)

@@ -272,9 +272,10 @@ def tile_modelgraphpolicy_pb_t_kernel(tc, xum, action, up_w3, up_b3, dyn_w1_mu, 
         make_identity(nc, ident[:])
 
         nc.sync.dma_start(out=x_all[:, 0:2, :], in_=x_v[:, 0:2, :])
-        nc.sync.dma_start(out=brow3[0:1, :], in_=up_b3.unsqueeze(0))
         for lo, hi in ((0, 2), (2, 4), (4, 7)):
             nc.sync.dma_start(out=w3_raw[:, lo:hi, :], in_=w3_v[:, lo:hi, :])
+            if lo == 0:
+                nc.sync.dma_start(out=brow3[0:1, :], in_=up_b3.unsqueeze(0))
         nc.sync.dma_start(out=x_all[:, 2:4, :], in_=x_v[:, 2:4, :])
         nc.sync.dma_start(out=x_all[:, 4:8, :], in_=x_v[:, 4:8, :])
         nc.sync.dma_start(out=w1_raw[:], in_=dyn_w1_mu.rearrange("(r p) k -> p r k", p=P))
@@ -285,7 +286,7 @@ def tile_modelgraphpolicy_pb_t_kernel(tc, xum, action, up_w3, up_b3, dyn_w1_mu, 
         nc.sync.dma_start(out=x_all[:, 16:24, :], in_=x_v[:, 16:24, :])
         nc.sync.dma_start(out=x_all[:, 24:32, :], in_=x_v[:, 24:32, :])
 
-        keep_clock(5)
+        keep_clock(4)
         tr_x(0)
         ex_x(0)
         tr_w3(0, ps_t, "t")
@@ -403,11 +404,11 @@ def tile_modelgraphpolicy_pb_t_kernel(tc, xum, action, up_w3, up_b3, dyn_w1_mu, 
             if k + 2 < NP:
                 q_x(k + 2)
             if k > 3:
-                relu_v(k - 4, 0, 448)
-                relu_s(k - 4, 448, 704)
+                relu_v(k - 4, 0, 384)
+                relu_s(k - 4, 384, 672)
             root(k)
             if k > 3:
-                relu_s(k - 4, 704, 2 * F1)
+                relu_s(k - 4, 672, 2 * F1)
                 store(k - 4, 0, 2)
 
         ex_m(NP - 2)

@@ -20,6 +20,8 @@ NW3 = M // P
 NW1 = F1 // P
 K2 = M + A
 RMAX = 1e12
+RS = 576
+FMAX = 3.4028234663852886e38
 
 FLOPS = 2 * B * H * M + 2 * B * (M + A) * F1
 
@@ -55,7 +57,7 @@ def tile_modelgraphpolicy_pb_t_kernel(tc, xum, action, up_w3, up_b3, dyn_w1_mu, 
         xc = keep.tile([P, NT, P], U32, name="xc", align_bytes=64)
         xs = keep.tile([P, NT, P], U8, name="xs", align_bytes=64)
         ss = keep.tile([P, NT], F32, name="ss")
-        nrm = keep.tile([P, NT], F32, name="nrm")
+        nrm = keep.tile([P, NT, 2], F32, name="nrm")
         rn = keep.tile([P, NT], F32, name="rn")
 
         x_v = xum.rearrange("(p i) k -> p i k", i=NT)
@@ -176,11 +178,13 @@ def tile_modelgraphpolicy_pb_t_kernel(tc, xum, action, up_w3, up_b3, dyn_w1_mu, 
 
         def root(k):
             nc.scalar.activation(
-                out=nrm[:, 2 * k : 2 * k + 2], in_=ss[:, 2 * k : 2 * k + 2], func=ACT.Abs_reciprocal_sqrt
+                out=nrm[:, 2 * k : 2 * k + 2, 0], in_=ss[:, 2 * k : 2 * k + 2], func=ACT.Abs_reciprocal_sqrt
             )
 
         def norm_factor(k):
-            nc.vector.tensor_scalar_min(out=rn[:, 2 * k : 2 * k + 2], in0=nrm[:, 2 * k : 2 * k + 2], scalar1=RMAX)
+            nc.vector.tensor_reduce(
+                out=rn[:, 2 * k : 2 * k + 2], in_=nrm[:, 2 * k : 2 * k + 2, :], op=ALU.min, axis=mybir.AxisListType.X
+            )
 
         def scale(i, engine):
             engine.tensor_scalar(
@@ -262,11 +266,18 @@ def tile_modelgraphpolicy_pb_t_kernel(tc, xum, action, up_w3, up_b3, dyn_w1_mu, 
             cols = pair_columns(k, lo, hi)
             nc.vector.tensor_scalar_max(out=cols, in0=cols, scalar1=0.0)
 
+        def relu_g(k, lo, hi):
+            cols = pair_columns(k, lo, hi)
+            nc.gpsimd.tensor_scalar(
+                out=cols, in0=cols, scalar1=FMAX, scalar2=0.0, op0=ALU.min, op1=ALU.max
+            )
+
         def store(k, lo, hi):
             nc.sync.dma_start(out=o_v[:, 2 * k + lo : 2 * k + hi, :], in_=live["ot", k][:, lo:hi, :])
 
         nc.vector.memset(brow3[:].bitcast(I32), 0)
         nc.vector.memset(warm[:], 1.0)
+        nc.vector.memset(nrm[:, :, 1], RMAX)
         nc.vector.memset(ones[:], 1.0)
         nc.scalar.activation(out=warm[:], in_=warm[:], func=ACT.Abs_reciprocal_sqrt)
         make_identity(nc, ident[:])
@@ -373,9 +384,10 @@ def tile_modelgraphpolicy_pb_t_kernel(tc, xum, action, up_w3, up_b3, dyn_w1_mu, 
         q_m(0)
         q_x(4)
 
+        norm_factor(2)
+
         for k in range(3, NP):
             a, b = 2 * k, 2 * k + 1
-            norm_factor(k - 1)
             add_hi(a)
             stage2(a - 6)
             stage2(b - 6)
@@ -391,6 +403,8 @@ def tile_modelgraphpolicy_pb_t_kernel(tc, xum, action, up_w3, up_b3, dyn_w1_mu, 
             squares(a)
             squares(b)
             normalise(k - 1)
+            if k > 3:
+                relu_g(k - 4, RS, 2 * F1)
             if k + 1 < NP:
                 z_hi(a + 2)
                 z_lo(b + 2)
@@ -400,19 +414,18 @@ def tile_modelgraphpolicy_pb_t_kernel(tc, xum, action, up_w3, up_b3, dyn_w1_mu, 
                 tr_x(k + 3)
             if k + 1 < NP:
                 z_hi(b + 2)
+            if k > 3:
+                relu_s(k - 4, 0, RS // 2)
+            root(k)
             q_m(k - 2)
+            norm_factor(k)
             if k + 2 < NP:
                 q_x(k + 2)
             if k > 3:
-                relu_v(k - 4, 0, 384)
-                relu_s(k - 4, 384, 672)
-            root(k)
-            if k > 3:
-                relu_s(k - 4, 672, 2 * F1)
+                relu_s(k - 4, RS // 2, RS)
                 store(k - 4, 0, 2)
 
         ex_m(NP - 2)
-        norm_factor(NP - 1)
         normalise(NP - 1)
         stage2(NT - 6)
         stage2(NT - 5)

@@ -20,7 +20,7 @@ NW3 = M // P
 NW1 = F1 // P
 K2 = M + A
 RMAX = 1e12
-RS = 576
+RS = 512
 FMAX = 3.4028234663852886e38
 
 FLOPS = 2 * B * H * M + 2 * B * (M + A) * F1
@@ -390,10 +390,10 @@ def tile_modelgraphpolicy_pb_t_kernel(tc, xum, action, up_w3, up_b3, dyn_w1_mu, 
             a, b = 2 * k, 2 * k + 1
             add_hi(a)
             stage2(a - 6)
-            stage2(b - 6)
             add_b3(b)
+            if k > 3:
+                add_b1(b - 8)
             add_b1(a - 6)
-            add_b1(b - 6)
             if k + 1 < NP:
                 z_lo(a + 2)
                 add_lo(a + 2)
@@ -408,6 +408,7 @@ def tile_modelgraphpolicy_pb_t_kernel(tc, xum, action, up_w3, up_b3, dyn_w1_mu, 
             if k + 1 < NP:
                 z_hi(a + 2)
                 z_lo(b + 2)
+            stage2(b - 6)
             tr_m(a - 2)
             tr_m(b - 2)
             if k + 3 < NP:
@@ -425,6 +426,7 @@ def tile_modelgraphpolicy_pb_t_kernel(tc, xum, action, up_w3, up_b3, dyn_w1_mu, 
                 relu_s(k - 4, RS // 2, RS)
                 store(k - 4, 0, 2)
 
+        add_b1(NT - 7)
         ex_m(NP - 2)
         normalise(NP - 1)
         stage2(NT - 6)

@@ -67,7 +67,12 @@ def tile_modelgraphpolicy_pb_t_kernel(tc, xum, action, up_w3, up_b3, dyn_w1_mu, 
 
         live = {}
 
-        def transpose_words(bank, sources):
+        def keep_clock(bank, n):
+            for r in range(n):
+                nc.tensor.matmul(out=bank, lhsT=ones[:, 0:P], rhs=ones[:], start=True, stop=True)
+
+        def transpose_words(bank, sources, warm=0):
+            keep_clock(bank[:].rearrange("p s n -> p (s n)"), warm)
             for s, src in enumerate(sources):
                 nc.tensor.transpose(out=bank[:, s, :], in_=src, identity=ident[:])
 
@@ -84,11 +89,12 @@ def tile_modelgraphpolicy_pb_t_kernel(tc, xum, action, up_w3, up_b3, dyn_w1_mu, 
             words = row.bitcast(F32)
             return [words[:, 0:128], words[:, 128:256], words[:, 256:512:2], words[:, 257:512:2]]
 
-        def tr_x(k):
+        def tr_x(k, warm=0):
             bank = ps_t.tile([P, 4, P], F32, name="tx%d" % k, tag="t")
             transpose_words(
                 bank,
                 [x_all[:, 2 * k + a, :].bitcast(F32)[:, P * u : P * u + P] for a in range(2) for u in range(2)],
+                warm,
             )
             live["tx", k] = bank
 
@@ -104,12 +110,13 @@ def tile_modelgraphpolicy_pb_t_kernel(tc, xum, action, up_w3, up_b3, dyn_w1_mu, 
                 xs[:, 2 * k : 2 * k + 2, :].rearrange("p a n -> p (a n)"),
             )
 
-        def tr_w3(k, pool, tag):
+        def tr_w3(k, pool, tag, warm=0):
             n = min(2, NW3 - 2 * k)
             bank = pool.tile([P, 4, P], F32, name="tw3%d" % k, tag=tag)
             transpose_words(
                 bank,
                 [w3_raw[:, 2 * k + a, :].bitcast(F32)[:, P * u : P * u + P] for a in range(n) for u in range(2)],
+                warm,
             )
             live["tw3", k] = bank
 
@@ -123,14 +130,9 @@ def tile_modelgraphpolicy_pb_t_kernel(tc, xum, action, up_w3, up_b3, dyn_w1_mu, 
             nc.tensor.matmul(out=bank[:, 0:n], lhsT=ones[:, 0:P], rhs=row, start=True, stop=True)
             copy(out=wide, in_=bank[:, 0:n])
 
-        def keep_clock(n):
-            bank = ps_o.tile([P, 512], F32, name="clock", tag="o")
-            for r in range(n):
-                nc.tensor.matmul(out=bank[:], lhsT=ones[:, 0:P], rhs=ones[:], start=True, stop=True)
-
-        def tr_w1(r):
+        def tr_w1(r, warm=0):
             bank = ps_o.tile([P, 4, P], F32, name="tw1%d" % r, tag="o")
-            transpose_words(bank, row_words(w1_raw[:, r, :]))
+            transpose_words(bank, row_words(w1_raw[:, r, :]), warm)
             live["tw1", r] = bank
 
         def ex_w1(r, copy):
@@ -200,9 +202,9 @@ def tile_modelgraphpolicy_pb_t_kernel(tc, xum, action, up_w3, up_b3, dyn_w1_mu, 
             for i in (2 * k, 2 * k + 1):
                 scale(i, nc.gpsimd if k < NP - 1 else nc.vector)
 
-        def tr_m(i):
+        def tr_m(i, warm=0):
             bank = ps_t.tile([P, 4, P], F32, name="tm%d" % i, tag="t")
-            transpose_words(bank, row_words(mu_all[:, i, :]))
+            transpose_words(bank, row_words(mu_all[:, i, :]), warm)
             live["tm", i] = bank
 
         def ex_m1(k, a):
@@ -297,12 +299,11 @@ def tile_modelgraphpolicy_pb_t_kernel(tc, xum, action, up_w3, up_b3, dyn_w1_mu, 
         nc.sync.dma_start(out=x_all[:, 16:24, :], in_=x_v[:, 16:24, :])
         nc.sync.dma_start(out=x_all[:, 24:32, :], in_=x_v[:, 24:32, :])
 
-        keep_clock(4)
-        tr_x(0)
+        tr_x(0, 4)
         ex_x(0)
         tr_w3(0, ps_t, "t")
         ex_w3(0, nc.vector.tensor_copy)
-        tr_w3(1, ps_t, "t")
+        tr_w3(1, ps_t, "t", 2)
         ex_w3(1, nc.scalar.copy)
         q_x(0)
         quantise(w3g[:, 0:2, :, :].rearrange("p a n t -> p (a n t)"), w3c[:, 0:256], w3s[:, 0:256])
@@ -311,7 +312,7 @@ def tile_modelgraphpolicy_pb_t_kernel(tc, xum, action, up_w3, up_b3, dyn_w1_mu, 
         quantise(w3g[:, 2:4, :, :].rearrange("p a n t -> p (a n t)"), w3c[:, 256:512], w3s[:, 256:512])
         tr_w3(2, ps_z, "z")
         ex_w3(2, nc.scalar.copy)
-        tr_w3(3, ps_z, "z")
+        tr_w3(3, ps_z, "z", 1)
         ex_w3(3, nc.vector.tensor_copy)
         tr_x(1)
         z_lo(0)
@@ -336,7 +337,7 @@ def tile_modelgraphpolicy_pb_t_kernel(tc, xum, action, up_w3, up_b3, dyn_w1_mu, 
 
         add_b3(2)
         z_hi(3)
-        tr_w1(0)
+        tr_w1(0, 1)
         tr_w1(1)
         add_b3(3)
         q_x(2)
@@ -353,17 +354,19 @@ def tile_modelgraphpolicy_pb_t_kernel(tc, xum, action, up_w3, up_b3, dyn_w1_mu, 
         z_lo(5)
         ex_w1(1, nc.vector.tensor_copy)
         add_lo(4)
-        z_hi(5)
         tr_w1(2)
         tr_w1(3)
-        tr_m(0)
-        tr_m(1)
-        tr_x(4)
+        z_hi(5)
         add_hi(4)
-
+        z_lo(6)
         squares(4)
         norm_factor(1)
-        add_b3(5)
+        add_lo(5)
+        add_hi(5)
+        tr_m(0, 1)
+        tr_m(1)
+        tr_x(4)
+
         normalise(1)
         ex_m1(0, 0)
         squares(5)
@@ -372,18 +375,17 @@ def tile_modelgraphpolicy_pb_t_kernel(tc, xum, action, up_w3, up_b3, dyn_w1_mu, 
         ex_x(4)
         ex_w1(2, nc.vector.tensor_copy)
         ex_w1(3, nc.vector.tensor_copy)
-        z_a(3)
+        z_hi(6)
         z_lo(7)
         add_lo(6)
-        tr_m(2)
-        tr_m(3)
+        tr_m(2, 1)
+        tr_m(3, 2)
         tr_x(5)
         z_hi(7)
         for c in range(2):
             quantise(w1g[:, c, :, :].rearrange("p f t -> p (f t)"), w1c[:, c, :], w1s[:, c, :])
         q_m(0)
         q_x(4)
-
         norm_factor(2)
 
         for k in range(3, NP):

@@ -20,6 +20,7 @@ NW3 = M // P
 NW1 = F1 // P
 K2 = M + A
 RMAX = 1e12
+RV = 128
 RS = 512
 FMAX = 3.4028234663852886e38
 
@@ -41,7 +42,7 @@ def tile_modelgraphpolicy_pb_t_kernel(tc, xum, action, up_w3, up_b3, dyn_w1_mu, 
         ident = keep.tile([P, P], F32, name="ident")
         ones = keep.tile([P, 512], BF16, name="ones")
         brow3 = keep.tile([P, M], BF16, name="brow3")
-        bias3 = keep.tile([P, M], F32, name="bias3")
+        bias3 = keep.tile([P, M], BF16, name="bias3")
         bias1 = keep.tile([P, F1], BF16, name="bias1")
         warm = keep.tile([P, 1], F32, name="warm")
         x_all = keep.tile([P, NT, H], BF16, name="x_all")
@@ -124,11 +125,11 @@ def tile_modelgraphpolicy_pb_t_kernel(tc, xum, action, up_w3, up_b3, dyn_w1_mu, 
             n = min(2, NW3 - 2 * k)
             leave_bank(copy, w3g[:, 2 * k : 2 * k + n, :, :], live["tw3", k], n)
 
-        def spread(row, wide, copy):
-            bank = ps_o.tile([P, 512], F32, name="spread", tag="o")
-            n = row.shape[1]
-            nc.tensor.matmul(out=bank[:, 0:n], lhsT=ones[:, 0:P], rhs=row, start=True, stop=True)
-            copy(out=wide, in_=bank[:, 0:n])
+        def spread_b3():
+            bank = ps_o.tile([P, M], BF16, name="spread", tag="o")
+            for lo, hi in ((0, 512), (512, M)):
+                nc.tensor.matmul(out=bank[:, lo:hi], lhsT=ones[:, 0:P], rhs=brow3[:, lo:hi], start=True, stop=True)
+            nc.scalar.copy(out=bias3[:], in_=bank[:])
 
         def tr_w1(r, warm=0):
             bank = ps_o.tile([P, 4, P], F32, name="tw1%d" % r, tag="o")
@@ -303,19 +304,18 @@ def tile_modelgraphpolicy_pb_t_kernel(tc, xum, action, up_w3, up_b3, dyn_w1_mu, 
         ex_x(0)
         tr_w3(0, ps_t, "t")
         ex_w3(0, nc.vector.tensor_copy)
-        tr_w3(1, ps_t, "t", 2)
+        tr_w3(1, ps_t, "t")
         ex_w3(1, nc.scalar.copy)
         q_x(0)
         quantise(w3g[:, 0:2, :, :].rearrange("p a n t -> p (a n t)"), w3c[:, 0:256], w3s[:, 0:256])
-        spread(brow3[:, 0:512], bias3[:, 0:512], nc.vector.tensor_copy)
-        spread(brow3[:, 512:M], bias3[:, 512:M], nc.scalar.copy)
-        quantise(w3g[:, 2:4, :, :].rearrange("p a n t -> p (a n t)"), w3c[:, 256:512], w3s[:, 256:512])
         tr_w3(2, ps_z, "z")
         ex_w3(2, nc.scalar.copy)
-        tr_w3(3, ps_z, "z", 1)
+        tr_w3(3, ps_z, "z")
+        quantise(w3g[:, 2:4, :, :].rearrange("p a n t -> p (a n t)"), w3c[:, 256:512], w3s[:, 256:512])
         ex_w3(3, nc.vector.tensor_copy)
-        tr_x(1)
+        spread_b3()
         z_lo(0)
+        tr_x(1)
         quantise(w3g[:, 4:6, :, :].rearrange("p a n t -> p (a n t)"), w3c[:, 512:768], w3s[:, 512:768])
         quantise(w3g[:, 6:7, :, :].rearrange("p a n t -> p (a n t)"), w3c[:, 768:896], w3s[:, 768:896])
         ex_x(1)
@@ -324,8 +324,8 @@ def tile_modelgraphpolicy_pb_t_kernel(tc, xum, action, up_w3, up_b3, dyn_w1_mu, 
         tr_x(2)
 
         add_lo(0)
-        q_x(1)
         add_hi(0)
+        q_x(1)
         z_hi(1)
         squares(0)
         ex_x(2)
@@ -337,7 +337,7 @@ def tile_modelgraphpolicy_pb_t_kernel(tc, xum, action, up_w3, up_b3, dyn_w1_mu, 
 
         add_b3(2)
         z_hi(3)
-        tr_w1(0, 1)
+        tr_w1(0)
         tr_w1(1)
         add_b3(3)
         q_x(2)
@@ -363,7 +363,7 @@ def tile_modelgraphpolicy_pb_t_kernel(tc, xum, action, up_w3, up_b3, dyn_w1_mu, 
         norm_factor(1)
         add_lo(5)
         add_hi(5)
-        tr_m(0, 1)
+        tr_m(0)
         tr_m(1)
         tr_x(4)
 
@@ -375,11 +375,11 @@ def tile_modelgraphpolicy_pb_t_kernel(tc, xum, action, up_w3, up_b3, dyn_w1_mu, 
         ex_x(4)
         ex_w1(2, nc.vector.tensor_copy)
         ex_w1(3, nc.vector.tensor_copy)
+        add_lo(6)
         z_hi(6)
         z_lo(7)
-        add_lo(6)
-        tr_m(2, 1)
-        tr_m(3, 2)
+        tr_m(2)
+        tr_m(3)
         tr_x(5)
         z_hi(7)
         for c in range(2):
@@ -418,25 +418,27 @@ def tile_modelgraphpolicy_pb_t_kernel(tc, xum, action, up_w3, up_b3, dyn_w1_mu, 
             if k + 1 < NP:
                 z_hi(b + 2)
             if k > 3:
-                relu_s(k - 4, 0, RS // 2)
+                relu_s(k - 4, RV, (RV + RS) // 2)
             root(k)
             q_m(k - 2)
+            if k == NP - 1:
+                add_b1(b - 6)
             norm_factor(k)
             if k + 2 < NP:
                 q_x(k + 2)
             if k > 3:
-                relu_s(k - 4, RS // 2, RS)
+                relu_v(k - 4, 0, RV)
+                relu_s(k - 4, (RV + RS) // 2, RS)
                 store(k - 4, 0, 2)
 
-        add_b1(NT - 7)
         ex_m(NP - 2)
         normalise(NP - 1)
         stage2(NT - 6)
         stage2(NT - 5)
         tr_m(NT - 2)
         tr_m(NT - 1)
-        q_m(NP - 2)
         add_b1(NT - 6)
+        q_m(NP - 2)
         add_b1(NT - 5)
         relu_s(NP - 4, 0, F1)
         relu_s(NP - 4, F1, 2 * F1)

from contextlib import ExitStack

import concourse.mybir as mybir
from concourse.masks import make_identity

F32 = mybir.dt.float32
BF16 = mybir.dt.bfloat16
U32 = mybir.dt.uint32
U8 = mybir.dt.uint8
I32 = mybir.dt.int32
FP8X4 = mybir.dt.float8_e4m3fn_x4
ALU = mybir.AluOpType
ACT = mybir.ActivationFunctionType

P = 128
B, H, A, M, F1 = 4096, 512, 128, 896, 512
NT = B // P
NP = NT // 2
NW3 = M // P
NW1 = F1 // P
K2 = M + A
RMAX = 1e12
RV = 128
RS = 512
FMAX = 3.4028234663852886e38

FLOPS = 2 * B * H * M + 2 * B * (M + A) * F1


def tile_modelgraphpolicy_pb_t_kernel(tc, xum, action, up_w3, up_b3, dyn_w1_mu, dyn_b1, out):
    nc = tc.nc
    with ExitStack() as ctx:
        keep = ctx.enter_context(tc.tile_pool(name="keep", bufs=1))
        two = ctx.enter_context(tc.tile_pool(name="two", bufs=2))
        four = ctx.enter_context(tc.tile_pool(name="four", bufs=4))
        six = ctx.enter_context(tc.tile_pool(name="six", bufs=6))
        ps_z = ctx.enter_context(tc.psum_pool(name="ps_z", bufs=3))
        ps_t = ctx.enter_context(tc.psum_pool(name="ps_t", bufs=3))
        ps_o = ctx.enter_context(tc.psum_pool(name="ps_o", bufs=2))
        ctx.enter_context(tc.manual_schedule())

        ident = keep.tile([P, P], F32, name="ident")
        ones = keep.tile([P, 512], BF16, name="ones")
        brow3 = keep.tile([P, M], BF16, name="brow3")
        bias3 = keep.tile([P, M], BF16, name="bias3")
        bias1 = keep.tile([P, F1], BF16, name="bias1")
        warm = keep.tile([P, 1], F32, name="warm")
        x_all = keep.tile([P, NT, H], BF16, name="x_all")
        w3_raw = keep.tile([P, NW3, H], BF16, name="w3_raw")
        w1_raw = keep.tile([P, NW1, K2], BF16, name="w1_raw")
        w3g = keep.tile([P, NW3, P, 4], BF16, name="w3g", align_bytes=64)
        w1g = keep.tile([P, 2, F1, 4], BF16, name="w1g", align_bytes=64)
        w3c = keep.tile([P, M], U32, name="w3c", align_bytes=64)
        w3s = keep.tile([P, M], U8, name="w3s", align_bytes=64)
        w1c = keep.tile([P, 2, F1], U32, name="w1c", align_bytes=64)
        w1s = keep.tile([P, 2, F1], U8, name="w1s", align_bytes=64)
        mu_all = keep.tile([P, NT, K2], BF16, name="mu_all")
        xc = keep.tile([P, NT, P], U32, name="xc", align_bytes=64)
        xs = keep.tile([P, NT, P], U8, name="xs", align_bytes=64)
        ss = keep.tile([P, NT], F32, name="ss")
        nrm = keep.tile([P, NT, 2], F32, name="nrm")
        rn = keep.tile([P, NT], F32, name="rn")

        x_v = xum.rearrange("(p i) k -> p i k", i=NT)
        a_v = action.rearrange("(p i) a -> p i a", i=NT)
        o_v = out.rearrange("(p i) f -> p i f", i=NT)
        w3_v = up_w3.rearrange("(j p) k -> p j k", p=P)

        live = {}

        def keep_clock(bank, n):
            for r in range(n):
                nc.tensor.matmul(out=bank, lhsT=ones[:, 0:P], rhs=ones[:], start=True, stop=True)

        def transpose_words(bank, sources, warm=0):
            keep_clock(bank[:].rearrange("p s n -> p (s n)"), warm)
            for s, src in enumerate(sources):
                nc.tensor.transpose(out=bank[:, s, :], in_=src, identity=ident[:])

        def leave_bank(copy, grouped, bank, pairs):
            copy(
                out=grouped.bitcast(F32),
                in_=bank[:, 0 : 2 * pairs, :].rearrange("p (a u) n -> p a n u", u=2),
            )

        def quantise(grouped, codes, scales):
            nc.vector.quantize_mx(out=codes.bitcast(FP8X4), scales=scales, in_=grouped)

        def row_words(row):
            words = row.bitcast(F32)
            return [words[:, 0:128], words[:, 128:256], words[:, 256:512:2], words[:, 257:512:2]]

        def tr_x(k, warm=0):
            bank = ps_t.tile([P, 4, P], F32, name="tx%d" % k, tag="t")
            transpose_words(
                bank,
                [x_all[:, 2 * k + a, :].bitcast(F32)[:, P * u : P * u + P] for a in range(2) for u in range(2)],
                warm,
            )
            live["tx", k] = bank

        def ex_x(k):
            xg = two.tile([P, 2, P, 4], BF16, name="xg%d" % k, tag="xg", align_bytes=64)
            leave_bank(nc.scalar.copy, xg[:], live["tx", k], 2)
            live["xg", k] = xg

        def q_x(k):
            quantise(
                live["xg", k][:].rearrange("p a n t -> p (a n t)"),
                xc[:, 2 * k : 2 * k + 2, :].rearrange("p a n -> p (a n)"),
                xs[:, 2 * k : 2 * k + 2, :].rearrange("p a n -> p (a n)"),
            )

        def tr_w3(k, pool, tag, warm=0):
            n = min(2, NW3 - 2 * k)
            bank = pool.tile([P, 4, P], F32, name="tw3%d" % k, tag=tag)
            transpose_words(
                bank,
                [w3_raw[:, 2 * k + a, :].bitcast(F32)[:, P * u : P * u + P] for a in range(n) for u in range(2)],
                warm,
            )
            live["tw3", k] = bank

        def ex_w3(k, copy):
            n = min(2, NW3 - 2 * k)
            leave_bank(copy, w3g[:, 2 * k : 2 * k + n, :, :], live["tw3", k], n)

        def spread_b3():
            bank = ps_o.tile([P, M], BF16, name="spread", tag="o")
            for lo, hi in ((0, 512), (512, M)):
                nc.tensor.matmul(out=bank[:, lo:hi], lhsT=ones[:, 0:P], rhs=brow3[:, lo:hi], start=True, stop=True)
            nc.scalar.copy(out=bias3[:], in_=bank[:])

        def tr_w1(r, warm=0):
            bank = ps_o.tile([P, 4, P], F32, name="tw1%d" % r, tag="o")
            transpose_words(bank, row_words(w1_raw[:, r, :]), warm)
            live["tw1", r] = bank

        def ex_w1(r, copy):
            leave_bank(copy, w1g[:, :, P * r : P * r + P, :], live["tw1", r], 2)

        def z_pass(i, dst, lo, hi):
            nc.tensor.matmul_mx(
                out=dst,
                lhsT=xc[:, i, :].bitcast(FP8X4),
                lhsT_scale=xs[:, i, :],
                rhs=w3c[:, lo:hi].bitcast(FP8X4),
                rhs_scale=w3s[:, lo:hi],
                start=True,
                stop=True,
            )

        def z_lo(i):
            live["za", i] = za = ps_z.tile([P, 512], F32, name="za%d" % i, tag="z")
            z_pass(i, za[:, 0:512], 0, 512)

        def z_hi(i):
            live["zc", i] = zc = ps_z.tile([P, 512], F32, name="zc%d" % i, tag="z")
            z_pass(i, zc[:, 0:256], 512, 768)
            z_pass(i, zc[:, 256:384], 768, 896)

        def add_lo(i):
            live["zb", i] = zb = six.tile([P, M], F32, name="zb%d" % i, tag="zb")
            nc.vector.tensor_tensor(out=zb[:, 0:512], in0=live["za", i][:], in1=bias3[:, 0:512], op=ALU.add)

        def add_hi(i):
            zb = live["zb", i]
            nc.vector.tensor_tensor(out=zb[:, 512:896], in0=live["zc", i][:, 0:384], in1=bias3[:, 512:896], op=ALU.add)

        def add_b3(i):
            add_lo(i)
            add_hi(i)

        def z_a(k):
            z_lo(2 * k)
            z_hi(2 * k)

        def squares(i):
            junk = two.tile([P, M], BF16, name="junk%d" % i, tag="junk")
            nc.scalar.activation(out=junk[:], in_=live["zb", i][:], func=ACT.Square, accum_out=ss[:, i : i + 1])

        def root(k):
            nc.scalar.activation(
                out=nrm[:, 2 * k : 2 * k + 2, 0], in_=ss[:, 2 * k : 2 * k + 2], func=ACT.Abs_reciprocal_sqrt
            )

        def norm_factor(k):
            nc.vector.tensor_reduce(
                out=rn[:, 2 * k : 2 * k + 2], in_=nrm[:, 2 * k : 2 * k + 2, :], op=ALU.min, axis=mybir.AxisListType.X
            )

        def scale(i, engine):
            engine.tensor_scalar(
                out=mu_all[:, i, 0:M],
                in0=live["zb", i][:],
                scalar1=rn[:, i : i + 1],
                scalar2=0.0,
                op0=ALU.mult,
                op1=ALU.add,
            )

        def normalise(k):
            for i in (2 * k, 2 * k + 1):
                scale(i, nc.gpsimd if k < NP - 1 else nc.vector)

        def tr_m(i, warm=0):
            bank = ps_t.tile([P, 4, P], F32, name="tm%d" % i, tag="t")
            transpose_words(bank, row_words(mu_all[:, i, :]), warm)
            live["tm", i] = bank

        def ex_m1(k, a):
            if a == 0:
                live["mug", k] = two.tile([P, 2, 2, P, 4], BF16, name="mug%d" % k, tag="mug", align_bytes=64)
            leave_bank(nc.scalar.copy, live["mug", k][:, a, :, :, :], live["tm", 2 * k + a], 2)

        def ex_m(k):
            ex_m1(k, 0)
            ex_m1(k, 1)

        def q_m(k):
            live["muc", k] = muc = two.tile([P, 2, 2, P], U32, name="muc%d" % k, tag="muc", align_bytes=64)
            live["mus", k] = mus = two.tile([P, 2, 2, P], U8, name="mus%d" % k, tag="mus", align_bytes=64)
            mug = live["mug", k]
            if k < NP - 1:
                quantise(
                    mug[:].rearrange("p a c n t -> p (a c n t)"),
                    muc[:].rearrange("p a c n -> p (a c n)"),
                    mus[:].rearrange("p a c n -> p (a c n)"),
                )
            else:
                for a in range(2):
                    quantise(
                        mug[:, a, :, :, :].rearrange("p c n t -> p (c n t)"),
                        muc[:, a, :, :].rearrange("p c n -> p (c n)"),
                        mus[:, a, :, :].rearrange("p c n -> p (c n)"),
                    )

        def stage2(i):
            k, a = divmod(i, 2)
            pool, tag = (ps_o, "o") if k < NP - 1 else (ps_z, "z")
            live["acc", i] = acc = pool.tile([P, F1], F32, name="acc%d" % i, tag=tag)
            for c in range(2):
                nc.tensor.matmul_mx(
                    out=acc[:],
                    lhsT=live["muc", k][:, a, c, :].bitcast(FP8X4),
                    lhsT_scale=live["mus", k][:, a, c, :],
                    rhs=w1c[:, c, :].bitcast(FP8X4),
                    rhs_scale=w1s[:, c, :],
                    start=(c == 0),
                    stop=(c == 1),
                )

        def add_b1(i):
            k, a = divmod(i, 2)
            if a == 0:
                live["ot", k] = four.tile([P, 2, F1], F32, name="ot%d" % k, tag="ot")
            nc.vector.tensor_tensor(
                out=live["ot", k][:, a, :], in0=live["acc", i][:], in1=bias1[:], op=ALU.add
            )

        def pair_columns(k, lo, hi):
            return live["ot", k][:].rearrange("p a f -> p (a f)")[:, lo:hi]

        def relu_s(k, lo, hi):
            cols = pair_columns(k, lo, hi)
            nc.scalar.activation(out=cols, in_=cols, func=ACT.Relu)

        def relu_v(k, lo, hi):
            cols = pair_columns(k, lo, hi)
            nc.vector.tensor_scalar_max(out=cols, in0=cols, scalar1=0.0)

        def relu_g(k, lo, hi):
            cols = pair_columns(k, lo, hi)
            nc.gpsimd.tensor_scalar(
                out=cols, in0=cols, scalar1=FMAX, scalar2=0.0, op0=ALU.min, op1=ALU.max
            )

        def store(k, lo, hi):
            nc.sync.dma_start(out=o_v[:, 2 * k + lo : 2 * k + hi, :], in_=live["ot", k][:, lo:hi, :])

        nc.vector.memset(brow3[:].bitcast(I32), 0)
        nc.vector.memset(warm[:], 1.0)
        nc.vector.memset(nrm[:, :, 1], RMAX)
        nc.vector.memset(ones[:], 1.0)
        nc.scalar.activation(out=warm[:], in_=warm[:], func=ACT.Abs_reciprocal_sqrt)
        make_identity(nc, ident[:])

        nc.sync.dma_start(out=x_all[:, 0:2, :], in_=x_v[:, 0:2, :])
        for lo, hi in ((0, 2), (2, 4), (4, 7)):
            nc.sync.dma_start(out=w3_raw[:, lo:hi, :], in_=w3_v[:, lo:hi, :])
            if lo == 0:
                nc.sync.dma_start(out=brow3[0:1, :], in_=up_b3.unsqueeze(0))
        nc.sync.dma_start(out=x_all[:, 2:4, :], in_=x_v[:, 2:4, :])
        nc.sync.dma_start(out=x_all[:, 4:8, :], in_=x_v[:, 4:8, :])
        nc.sync.dma_start(out=w1_raw[:], in_=dyn_w1_mu.rearrange("(r p) k -> p r k", p=P))
        nc.sync.dma_start(out=mu_all[:, 0:8, M:K2], in_=a_v[:, 0:8, :])
        nc.sync.dma_start(out=x_all[:, 8:16, :], in_=x_v[:, 8:16, :])
        nc.sync.dma_start(out=bias1[:], in_=dyn_b1.partition_broadcast(P))
        nc.sync.dma_start(out=mu_all[:, 8:NT, M:K2], in_=a_v[:, 8:NT, :])
        nc.sync.dma_start(out=x_all[:, 16:24, :], in_=x_v[:, 16:24, :])
        nc.sync.dma_start(out=x_all[:, 24:32, :], in_=x_v[:, 24:32, :])

        tr_x(0, 4)
        ex_x(0)
        tr_w3(0, ps_t, "t")
        ex_w3(0, nc.vector.tensor_copy)
        tr_w3(1, ps_t, "t")
        ex_w3(1, nc.scalar.copy)
        q_x(0)
        quantise(w3g[:, 0:2, :, :].rearrange("p a n t -> p (a n t)"), w3c[:, 0:256], w3s[:, 0:256])
        tr_w3(2, ps_z, "z")
        ex_w3(2, nc.scalar.copy)
        tr_w3(3, ps_z, "z")
        quantise(w3g[:, 2:4, :, :].rearrange("p a n t -> p (a n t)"), w3c[:, 256:512], w3s[:, 256:512])
        ex_w3(3, nc.vector.tensor_copy)
        spread_b3()
        z_lo(0)
        tr_x(1)
        quantise(w3g[:, 4:6, :, :].rearrange("p a n t -> p (a n t)"), w3c[:, 512:768], w3s[:, 512:768])
        quantise(w3g[:, 6:7, :, :].rearrange("p a n t -> p (a n t)"), w3c[:, 768:896], w3s[:, 768:896])
        ex_x(1)
        z_hi(0)
        z_lo(1)
        tr_x(2)

        add_lo(0)
        add_hi(0)
        q_x(1)
        z_hi(1)
        squares(0)
        ex_x(2)
        add_b3(1)
        squares(1)
        z_a(1)
        z_lo(3)
        tr_x(3)

        add_b3(2)
        z_hi(3)
        tr_w1(0)
        tr_w1(1)
        add_b3(3)
        q_x(2)
        ex_x(3)
        root(0)
        ex_w1(0, nc.vector.tensor_copy)
        squares(2)
        squares(3)
        root(1)
        norm_factor(0)
        q_x(3)
        normalise(0)
        z_a(2)
        z_lo(5)
        ex_w1(1, nc.vector.tensor_copy)
        add_lo(4)
        tr_w1(2)
        tr_w1(3)
        z_hi(5)
        add_hi(4)
        z_lo(6)
        squares(4)
        norm_factor(1)
        add_lo(5)
        add_hi(5)
        tr_m(0)
        tr_m(1)
        tr_x(4)

        normalise(1)
        ex_m1(0, 0)
        squares(5)
        ex_m1(0, 1)
        root(2)
        ex_x(4)
        ex_w1(2, nc.vector.tensor_copy)
        ex_w1(3, nc.vector.tensor_copy)
        add_lo(6)
        z_hi(6)
        z_lo(7)
        tr_m(2)
        tr_m(3)
        tr_x(5)
        z_hi(7)
        for c in range(2):
            quantise(w1g[:, c, :, :].rearrange("p f t -> p (f t)"), w1c[:, c, :], w1s[:, c, :])
        q_m(0)
        q_x(4)
        norm_factor(2)

        for k in range(3, NP):
            a, b = 2 * k, 2 * k + 1
            add_hi(a)
            stage2(a - 6)
            add_b3(b)
            if k > 3:
                add_b1(b - 8)
            add_b1(a - 6)
            if k + 1 < NP:
                z_lo(a + 2)
                add_lo(a + 2)
            ex_m(k - 2)
            if k + 2 < NP:
                ex_x(k + 2)
            squares(a)
            squares(b)
            normalise(k - 1)
            if k > 3:
                relu_g(k - 4, RS, 2 * F1)
            if k + 1 < NP:
                z_hi(a + 2)
                z_lo(b + 2)
            stage2(b - 6)
            tr_m(a - 2)
            tr_m(b - 2)
            if k + 3 < NP:
                tr_x(k + 3)
            if k + 1 < NP:
                z_hi(b + 2)
            if k > 3:
                relu_s(k - 4, RV, (RV + RS) // 2)
            root(k)
            q_m(k - 2)
            if k == NP - 1:
                add_b1(b - 6)
            norm_factor(k)
            if k + 2 < NP:
                q_x(k + 2)
            if k > 3:
                relu_v(k - 4, 0, RV)
                relu_s(k - 4, (RV + RS) // 2, RS)
                store(k - 4, 0, 2)

        ex_m(NP - 2)
        normalise(NP - 1)
        stage2(NT - 6)
        stage2(NT - 5)
        tr_m(NT - 2)
        tr_m(NT - 1)
        add_b1(NT - 6)
        q_m(NP - 2)
        add_b1(NT - 5)
        relu_s(NP - 4, 0, F1)
        relu_s(NP - 4, F1, 2 * F1)
        store(NP - 4, 0, 2)
        ex_m(NP - 1)
        q_m(NP - 1)
        stage2(NT - 4)
        stage2(NT - 3)
        add_b1(NT - 4)
        add_b1(NT - 3)
        relu_s(NP - 3, 0, F1)
        store(NP - 3, 0, 1)
        relu_s(NP - 3, F1, 2 * F1)
        store(NP - 3, 1, 2)
        stage2(NT - 2)
        stage2(NT - 1)
        add_b1(NT - 2)
        add_b1(NT - 1)
        relu_s(NP - 2, 0, F1)
        store(NP - 2, 0, 1)
        relu_s(NP - 2, F1, 2 * F1)
        store(NP - 2, 1, 2)
        relu_s(NP - 1, 0, F1)
        store(NP - 1, 0, 1)
        relu_v(NP - 1, F1, 2 * F1)
        store(NP - 1, 1, 2)
